import numpy as np
import ml_dtypes


def mxq(x, axis, fmt="e4m3"):
    dtype, down = {"e4m3": (ml_dtypes.float8_e4m3fn, 7), "e5m2": (ml_dtypes.float8_e5m2, 14)}[fmt]
    v = np.moveaxis(np.asarray(x, np.float32).astype(ml_dtypes.bfloat16).astype(np.float64), axis, -1)
    blocks = v.reshape(v.shape[:-1] + (-1, 32))
    amax = np.abs(blocks).max(-1, keepdims=True)
    byte = np.maximum(np.where(amax > 0, np.frexp(amax)[1] - 1 + 127, 0) - down, 1)
    scale = np.exp2(byte - 127.0)
    codes = (blocks / scale).astype(np.float32).astype(dtype).astype(np.float64)
    return np.moveaxis((codes * scale).reshape(v.shape), -1, axis)


WIDE = False


def mx_kscale(k):
    if not WIDE:
        return np.ones(k)
    levels = np.array([10, -10, 5, -5, 0])
    a = np.random.permutation(np.resize(levels, k // 512 * 4)).reshape(k // 512, 4)
    idx = np.arange(k)
    return np.exp2(a[idx // 512, idx % 128 // 32])


BF16 = ml_dtypes.bfloat16


def bf(x):
    return np.asarray(x, np.float32).astype(BF16)


def f64(x):
    return np.asarray(x).astype(np.float64)


B, M, D, N, P, H = 8, 1024, 512, 16, 8, 1024
R = B * P


def silu(v):
    return v / (1.0 + np.exp(-v))


def setup_inputs():
    s = mx_kscale(D)
    return {"xs_mix": bf(np.random.standard_normal((B, N, P, D)) * 0.3 / np.sqrt(D) * s),
            "task_emb": bf(np.random.standard_normal((P, D)) * 0.5 / np.sqrt(D) * s),
            "W1": bf(np.random.standard_normal((N, D, H)) * 2.0 / s[:, None]),
            "b1": bf(np.random.standard_normal((N, H)) * 0.3),
            "W2": bf(np.random.standard_normal((N, H, D)) / np.sqrt(H * D) * s),
            "b2": bf(np.random.standard_normal((N, D)) * 0.3 / np.sqrt(D) * s),
            "ln_g": bf(1.0 + 0.1 * np.random.standard_normal((N, D))),
            "ln_b": bf(0.1 * np.random.standard_normal((N, D)))}


def reference(xs_mix, task_emb, W1, b1, W2, b2, ln_g, ln_b):
    xs = f64(xs_mix) + f64(task_emb)[None, None, :, :]
    xe = xs.transpose(1, 0, 2, 3).reshape(N, R, D)
    h = silu((mxq(xe, 2, "e4m3") @ mxq(f64(W1), 1, "e4m3")) + f64(b1)[:, None, :])
    mlp = (mxq(h, 2, "e4m3") @ mxq(f64(W2), 1, "e4m3")) + f64(b2)[:, None, :]
    r = xe + mlp
    mu = r.mean(-1, keepdims=True)
    var = ((r - mu) ** 2).mean(-1, keepdims=True)
    ys = (r - mu) / np.sqrt(var + 1e-5) * f64(ln_g)[:, None, :] + f64(ln_b)[:, None, :]
    return ys.reshape(N, B, P, D).transpose(1, 0, 2, 3)

@@ -1,0 +1,385 @@
+from contextlib import ExitStack
+
+import concourse.mybir as mybir
+from concourse.masks import make_identity
+
+F32 = mybir.dt.float32
+BF16 = mybir.dt.bfloat16
+U32 = mybir.dt.uint32
+U8 = mybir.dt.uint8
+FP8X4 = mybir.dt.float8_e4m3fn_x4
+ALU = mybir.AluOpType
+ACT = mybir.ActivationFunctionType
+
+P = 128
+PACK = 4
+BATCH, EXPERTS, TASKS, D, H = 8, 16, 8, 512, 1024
+SLOTS = BATCH * TASKS
+PAIRS = EXPERTS // 2
+PAIR_ROWS = 2 * TASKS
+CHUNK = 512
+H_TILES = H // P
+K2_PASSES = H // (P * PACK)
+EPS = 1e-5
+
+VECTOR_COLS = 224
+RUN = 4
+
+TE_ROW, B2_ROW, G_ROW, B_ROW, B1_ROW = 0, 8, 32, 48, 64
+
+PREFETCH = 4
+DRAIN = 2
+
+FLOPS = 2 * EXPERTS * SLOTS * D * H * 2
+
+
+def regroup(nc, grouped, rows):
+    dst = grouped.rearrange("p (c i) j -> p c j i", i=RUN)
+    src = rows.rearrange("p j (c i) -> p c j i", i=RUN)
+    split = VECTOR_COLS // RUN
+    nc.vector.tensor_copy(out=dst[:, :split], in_=src[:, :split])
+    nc.scalar.copy(out=dst[:, split:], in_=src[:, split:])
+
+
+def quantise(nc, codes, scales, grouped):
+    nc.vector.quantize_mx(out=codes.bitcast(FP8X4), scales=scales, in_=grouped)
+
+
+def tile_hdmodel_pb_kernel(tc, xs_mix, task_emb, W1, b1, W2, b2, ln_g, ln_b, out):
+    nc = tc.nc
+    with ExitStack() as ctx:
+        const = ctx.enter_context(tc.tile_pool(name="const", bufs=1))
+        raw = ctx.enter_context(tc.tile_pool(name="raw", bufs=2 * (PREFETCH + 1)))
+        stage = ctx.enter_context(tc.tile_pool(name="stage", bufs=6))
+        wq = ctx.enter_context(tc.tile_pool(name="wq", bufs=8))
+        prep = ctx.enter_context(tc.tile_pool(name="prep", bufs=2))
+        hid = ctx.enter_context(tc.tile_pool(name="hid", bufs=2))
+        norm = ctx.enter_context(tc.tile_pool(name="norm", bufs=2))
+        ps_one = ctx.enter_context(tc.psum_pool(name="ps_one", bufs=1))
+        ps_two = ctx.enter_context(tc.psum_pool(name="ps_two", bufs=2))
+        ctx.enter_context(tc.manual_schedule())
+
+        w_chunks = {}
+        w_grouped = {}
+        w_packed = {}
+        xs_packed = {}
+        pair_tiles = {}
+        h_tiles = {}
+
+        def load_weights(n):
+            w1_raw = raw.tile([P, PACK, H], BF16, tag="raw")
+            nc.sync.dma_start(out=w1_raw[:], in_=W1[n].rearrange("(p j) h -> p j h", j=PACK))
+            w2_raw = raw.tile([P, K2_PASSES, PACK, D], BF16, tag="raw")
+            nc.sync.dma_start(
+                out=w2_raw[:].rearrange("p g t d -> p (g t) d"),
+                in_=W2[n].rearrange("(s p) d -> p s d", p=P),
+            )
+            for c in range(H // CHUNK):
+                w_chunks[(n, c)] = w1_raw[:, :, c * CHUNK : (c + 1) * CHUNK]
+            for g in range(K2_PASSES):
+                w_chunks[(n, 2 + g)] = w2_raw[:, g]
+
+        def regroup_chunk(n, c):
+            g_tile = stage.tile([P, CHUNK, PACK], BF16, tag="grouped", align_bytes=64)
+            regroup(nc, g_tile[:], w_chunks[(n, c)])
+            w_grouped[(n, c)] = g_tile
+
+        def quantise_chunk(n, c):
+            codes = wq.tile([P, CHUNK], U32, tag="codes", align_bytes=64)
+            scales = wq.tile([P, CHUNK], U8, tag="scales", align_bytes=64)
+            quantise(nc, codes[:], scales[:], w_grouped[(n, c)][:].rearrange("p w j -> p (w j)"))
+            w_packed[(n, c)] = (codes, scales)
+
+        x_all = const.tile([P, PAIRS, D], BF16)
+        for b in range(BATCH):
+            nc.sync.dma_start(
+                out=x_all[b * PAIR_ROWS : (b + 1) * PAIR_ROWS, :, :],
+                in_=xs_mix[b].rearrange("(i e) p d -> (e p) i d", e=2),
+            )
+        for n in range(PREFETCH):
+            load_weights(n)
+        vec_rows = const.tile([P, D], BF16)
+        nc.vector.memset(vec_rows[:], 0.0)
+        nc.scalar.dma_start(out=vec_rows[TE_ROW : TE_ROW + TASKS, :], in_=task_emb)
+        nc.scalar.dma_start(out=vec_rows[B2_ROW : B2_ROW + EXPERTS, :], in_=b2)
+        nc.scalar.dma_start(out=vec_rows[G_ROW : G_ROW + EXPERTS, :], in_=ln_g)
+        nc.scalar.dma_start(out=vec_rows[B_ROW : B_ROW + EXPERTS, :], in_=ln_b)
+        nc.scalar.dma_start(
+            out=vec_rows[B1_ROW : B1_ROW + 2 * EXPERTS, :],
+            in_=b1.rearrange("n (g c) -> (n g) c", g=K2_PASSES),
+        )
+
+        ident = const.tile([P, P], BF16)
+        make_identity(nc, ident[:])
+        neg_half = const.tile([P, 1], F32)
+        nc.gpsimd.memset(neg_half[:], -0.5)
+
+        h_grouped = []
+        for e in range(2):
+            h_tile = const.tile(
+                [P, K2_PASSES, BATCH, 2, TASKS, PACK], BF16, name="h_grouped%d" % e, align_bytes=64
+            )
+            nc.vector.memset(h_tile[:], 0.0)
+            h_grouped.append(h_tile)
+
+        vec_cols_ps = ps_one.tile([P, PACK, P], BF16, tag="flip")
+        for c in range(D // P):
+            nc.tensor.transpose(vec_cols_ps[:, c, :], vec_rows[:, c * P : (c + 1) * P], ident[:])
+        b1_col = const.tile([P, EXPERTS, K2_PASSES, PACK], F32)
+        nc.vector.tensor_copy(
+            out=b1_col[:],
+            in_=vec_cols_ps[:, :, B1_ROW : B1_ROW + 2 * EXPERTS].rearrange("q t (n g) -> q n g t", g=K2_PASSES),
+        )
+        gb_col = const.tile([P, 2, D // P, EXPERTS, TASKS], BF16)
+        for v in range(2):
+            first = G_ROW + v * EXPERTS
+            nc.vector.tensor_copy(
+                out=gb_col[:, v],
+                in_=vec_cols_ps[:, :, first : first + EXPERTS]
+                .unsqueeze(3)
+                .to_broadcast([P, D // P, EXPERTS, TASKS]),
+            )
+
+        sel_te = const.tile([P, BATCH, 2, TASKS], BF16)
+        nc.vector.tensor_copy(
+            out=sel_te[:].rearrange("q b e p -> q (b e) p"),
+            in_=ident[:, TE_ROW : TE_ROW + TASKS].unsqueeze(1).to_broadcast([P, BATCH * 2, TASKS]),
+        )
+        te_ps = ps_one.tile([P, D], F32, tag="spread")
+        nc.tensor.matmul(
+            te_ps[:], lhsT=sel_te[:].rearrange("q b e p -> q (b e p)"), rhs=vec_rows[:], start=True, stop=True
+        )
+        te_rep = const.tile([P, D], BF16)
+        nc.scalar.copy(out=te_rep[:], in_=te_ps[:])
+
+        def round_and_flip_xs(i):
+            xs16 = prep.tile([P, D], BF16)
+            nc.vector.tensor_tensor(out=xs16[:], in0=x_all[:, i, :], in1=te_rep[:], op=ALU.add)
+            xs_flip = ps_one.tile([P, PACK, P], BF16, tag="flip")
+            xs16_by_t = xs16[:].rearrange("r (q t) -> r t q", t=PACK)
+            for t in range(PACK):
+                nc.tensor.transpose(xs_flip[:, t, :], xs16_by_t[:, t, :], ident[:])
+            sel = prep.tile([P, BATCH, 2, TASKS], BF16)
+            nc.vector.tensor_tensor(
+                out=sel[:],
+                in0=sel_te[:],
+                in1=ident[:, B2_ROW + 2 * i : B2_ROW + 2 * i + 2]
+                .unsqueeze(1)
+                .unsqueeze(3)
+                .to_broadcast([P, BATCH, 2, TASKS]),
+                op=ALU.add,
+            )
+            teb2_ps = ps_one.tile([P, D], F32, tag="spread")
+            nc.tensor.matmul(
+                teb2_ps[:], lhsT=sel[:].rearrange("q b e p -> q (b e p)"), rhs=vec_rows[:], start=True, stop=True
+            )
+            pair_tiles[("xs_flip", i)] = xs_flip
+            pair_tiles[("teb2", i)] = teb2_ps
+
+        def group_xs(i):
+            xs_grouped = prep.tile([P, 2, BATCH, TASKS, PACK], BF16, align_bytes=64)
+            xs_flip_by_e = pair_tiles[("xs_flip", i)][:].rearrange("q t (b e p) -> q e b p t", e=2, p=TASKS)
+            for e in range(2):
+                nc.scalar.copy(out=xs_grouped[:, e], in_=xs_flip_by_e[:, e])
+            pair_tiles[("xs_grouped", i)] = xs_grouped
+
+        def residual_term(i):
+            resid = prep.tile([P, D], F32)
+            nc.vector.tensor_tensor(out=resid[:], in0=pair_tiles[("teb2", i)][:], in1=x_all[:, i, :], op=ALU.add)
+            pair_tiles[("resid", i)] = resid
+
+        def quantise_xs_and_spread_gain(i):
+            xs_codes = prep.tile([P, 2 * SLOTS], U32, align_bytes=64)
+            xs_scales = prep.tile([P, 2 * SLOTS], U8, align_bytes=64)
+            quantise(
+                nc, xs_codes[:], xs_scales[:], pair_tiles[("xs_grouped", i)][:].rearrange("q e b p t -> q (e b p t)")
+            )
+            xs_packed[i] = (xs_codes, xs_scales)
+            gb_wide = prep.tile([P, 2 * (D // P), BATCH, PAIR_ROWS], BF16)
+            nc.scalar.copy(
+                out=gb_wide[:],
+                in_=gb_col[:]
+                .rearrange("q v c n p -> q (v c) (n p)")[:, :, i * PAIR_ROWS : (i + 1) * PAIR_ROWS]
+                .unsqueeze(2)
+                .to_broadcast([P, 2 * (D // P), BATCH, PAIR_ROWS]),
+            )
+            gb_ps = ps_two.tile([P, 2, D], BF16, tag="gb")
+            for v in range(2):
+                for c in range(D // P):
+                    nc.tensor.transpose(
+                        gb_ps[:, v, c * P : (c + 1) * P],
+                        gb_wide[:, v * (D // P) + c].rearrange("q b s -> q (b s)"),
+                        ident[:],
+                    )
+            pair_tiles[("gb", i)] = gb_ps
+
+        def first_matmul(n, c):
+            if c == 0:
+                h_tiles[("h_ps", n)] = ps_two.tile([P, H_TILES, SLOTS], F32, tag="h", name="h_ps")
+            codes, scales = w_packed[(n, c)]
+            xs_codes, xs_scales = xs_packed[n // 2]
+            mine = slice((n % 2) * SLOTS, (n % 2 + 1) * SLOTS)
+            for m in range(CHUNK // P):
+                nc.tensor.matmul_mx(
+                    out=h_tiles[("h_ps", n)][:, c * (CHUNK // P) + m, :],
+                    lhsT=codes[:, m * P : (m + 1) * P].bitcast(FP8X4),
+                    lhsT_scale=scales[:, m * P : (m + 1) * P],
+                    rhs=xs_codes[:, mine].bitcast(FP8X4),
+                    rhs_scale=xs_scales[:, mine],
+                    start=True,
+                    stop=True,
+                )
+
+        def add_bias(n):
+            pre = hid.tile([P, K2_PASSES, BATCH, TASKS, PACK], F32)
+            nc.vector.tensor_tensor(
+                out=pre[:].rearrange("q g b p t -> q g (b p) t"),
+                in0=h_tiles[("h_ps", n)][:].rearrange("q (g t) r -> q g r t", t=PACK),
+                in1=b1_col[:, n].unsqueeze(2).to_broadcast([P, K2_PASSES, SLOTS, PACK]),
+                op=ALU.add,
+            )
+            h_tiles[("pre", n)] = pre
+
+        def silu(n):
+            e = n % 2
+            nc.scalar.activation(out=h_grouped[e][:, :, :, e, :, :], in_=h_tiles[("pre", n)][:], func=ACT.Silu)
+
+        def second_matmul(n):
+            i, e = divmod(n, 2)
+            h_codes = hid.tile([P, K2_PASSES * P], U32, align_bytes=64)
+            h_scales = hid.tile([P, K2_PASSES * P], U8, align_bytes=64)
+            quantise(nc, h_codes[:], h_scales[:], h_grouped[e][:].rearrange("q g b s p t -> q (g b s p t)"))
+            if e == 0:
+                pair_tiles[("mlp", i)] = ps_two.tile([P, D], F32, tag="mlp", name="mlp_ps")
+            for g in range(K2_PASSES):
+                codes, scales = w_packed[(n, 2 + g)]
+                nc.tensor.matmul_mx(
+                    out=pair_tiles[("mlp", i)][:],
+                    lhsT=h_codes[:, g * P : (g + 1) * P].bitcast(FP8X4),
+                    lhsT_scale=h_scales[:, g * P : (g + 1) * P],
+                    rhs=codes[:].bitcast(FP8X4),
+                    rhs_scale=scales[:],
+                    start=(e == 0 and g == 0),
+                    stop=(e == 1 and g == K2_PASSES - 1),
+                )
+
+        def add_residual(i):
+            r = norm.tile([P, D], F32)
+            r_sum = norm.tile([P, 1], F32)
+            nc.vector.scalar_tensor_tensor(
+                out=r[:],
+                in0=pair_tiles[("mlp", i)][:],
+                scalar=1.0,
+                in1=pair_tiles[("resid", i)][:],
+                op0=ALU.mult,
+                op1=ALU.add,
+                accum_out=r_sum[:],
+            )
+            neg_mean = norm.tile([P, 1], F32)
+            nc.gpsimd.tensor_scalar(
+                out=neg_mean[:], in0=r_sum[:], scalar1=-1.0 / D, scalar2=0.0, op0=ALU.mult, op1=ALU.add
+            )
+            pair_tiles[("r", i)] = r
+            pair_tiles[("neg_mean", i)] = neg_mean
+
+        def variance(i):
+            squares = norm.tile([P, D], F32)
+            sq_sum = norm.tile([P, 1], F32)
+            nc.scalar.activation(
+                out=squares[:],
+                in_=pair_tiles[("r", i)][:],
+                func=ACT.Square,
+                bias=pair_tiles[("neg_mean", i)][:],
+                scale=1.0,
+                accum_out=sq_sum[:],
+            )
+            var_eps = norm.tile([P, 1], F32)
+            nc.gpsimd.tensor_scalar(
+                out=var_eps[:], in0=sq_sum[:], scalar1=1.0 / D, scalar2=EPS, op0=ALU.mult, op1=ALU.add
+            )
+            rstd = norm.tile([P, 1], F32)
+            nc.gpsimd.tensor_tensor(out=rstd[:], in0=var_eps[:], in1=neg_half[:], op=ALU.pow)
+            pair_tiles[("rstd", i)] = rstd
+
+        def centre_times_gain(i):
+            scaled = norm.tile([P, D], F32)
+            nc.vector.scalar_tensor_tensor(
+                out=scaled[:],
+                in0=pair_tiles[("r", i)][:],
+                scalar=pair_tiles[("neg_mean", i)][:],
+                in1=pair_tiles[("gb", i)][:, 0, :],
+                op0=ALU.add,
+                op1=ALU.mult,
+            )
+            pair_tiles[("scaled", i)] = scaled
+
+        def normalise_and_store(i):
+            y = norm.tile([P, D], F32)
+            nc.vector.scalar_tensor_tensor(
+                out=y[:],
+                in0=pair_tiles[("scaled", i)][:],
+                scalar=pair_tiles[("rstd", i)][:],
+                in1=pair_tiles[("gb", i)][:, 1, :],
+                op0=ALU.mult,
+                op1=ALU.add,
+            )
+            for b in range(BATCH):
+                nc.sync.dma_start(
+                    out=out[b, 2 * i : 2 * i + 2].rearrange("e p d -> (e p) d"),
+                    in_=y[b * PAIR_ROWS : (b + 1) * PAIR_ROWS, :],
+                )
+
+        round_and_flip_xs(0)
+        group_xs(0)
+        residual_term(0)
+        quantise_xs_and_spread_gain(0)
+
+        for n in range(EXPERTS + DRAIN):
+            fresh = n < EXPERTS
+            behind = 1 <= n <= EXPERTS
+            even = n % 2 == 0
+            ending = n // 2 - 1
+            coming = (n + 1) // 2
+
+            if n + PREFETCH < EXPERTS:
+                load_weights(n + PREFETCH)
+            if behind:
+                quantise_chunk(n - 1, 2)
+            if fresh:
+                regroup_chunk(n, 0)
+            if behind:
+                add_bias(n - 1)
+            if even and 2 <= n < EXPERTS:
+                quantise_xs_and_spread_gain(coming)
+            if not even and n >= 3:
+                variance(ending)
+                centre_times_gain(ending)
+
+            if behind:
+                quantise_chunk(n - 1, 3)
+            if fresh:
+                regroup_chunk(n, 1)
+            if behind:
+                silu(n - 1)
+            if not even and coming < PAIRS:
+                round_and_flip_xs(coming)
+
+            if fresh:
+                quantise_chunk(n, 0)
+                first_matmul(n, 0)
+                regroup_chunk(n, 2)
+            if behind:
+                second_matmul(n - 1)
+            if not even and n >= 3:
+                normalise_and_store(ending)
+            if not even and coming < PAIRS:
+                group_xs(coming)
+
+            if fresh:
+                quantise_chunk(n, 1)
+                first_matmul(n, 1)
+                regroup_chunk(n, 3)
+            if even and n >= 2:
+                add_residual(ending)
+            if not even and coming < PAIRS:
+                residual_term(coming)

@@ -275,21 +275,20 @@ def tile_hdmodel_pb_kernel(tc, xs_mix, task_emb, W1, b1, W2, b2, ln_g, ln_b, out
                 op1=ALU.add,
                 accum_out=r_sum[:],
             )
-            neg_mean = norm.tile([P, 1], F32)
-            nc.gpsimd.tensor_scalar(
-                out=neg_mean[:], in0=r_sum[:], scalar1=-1.0 / D, scalar2=0.0, op0=ALU.mult, op1=ALU.add
-            )
             pair_tiles[("r", i)] = r
-            pair_tiles[("neg_mean", i)] = neg_mean
+            pair_tiles[("r_sum", i)] = r_sum
 
         def variance(i):
+            neg_mean = norm.tile([P, 1], F32)
+            nc.scalar.mul(neg_mean[:], pair_tiles[("r_sum", i)][:], -1.0 / D)
+            pair_tiles[("neg_mean", i)] = neg_mean
             squares = norm.tile([P, D], F32)
             sq_sum = norm.tile([P, 1], F32)
             nc.scalar.activation(
                 out=squares[:],
                 in_=pair_tiles[("r", i)][:],
                 func=ACT.Square,
-                bias=pair_tiles[("neg_mean", i)][:],
+                bias=neg_mean[:],
                 scale=1.0,
                 accum_out=sq_sum[:],
             )
@@ -353,7 +352,6 @@ def tile_hdmodel_pb_kernel(tc, xs_mix, task_emb, W1, b1, W2, b2, ln_g, ln_b, out
                 quantise_xs_and_spread_gain(coming)
             if not even and n >= 3:
                 variance(ending)
-                centre_times_gain(ending)
 
             if behind:
                 quantise_chunk(n - 1, 3)
@@ -367,11 +365,12 @@ def tile_hdmodel_pb_kernel(tc, xs_mix, task_emb, W1, b1, W2, b2, ln_g, ln_b, out
             if fresh:
                 quantise_chunk(n, 0)
                 first_matmul(n, 0)
-                regroup_chunk(n, 2)
             if behind:
                 second_matmul(n - 1)
+            if fresh:
+                regroup_chunk(n, 2)
             if not even and n >= 3:
-                normalise_and_store(ending)
+                centre_times_gain(ending)
             if not even and coming < PAIRS:
                 group_xs(coming)
 
@@ -383,3 +382,5 @@ def tile_hdmodel_pb_kernel(tc, xs_mix, task_emb, W1, b1, W2, b2, ln_g, ln_b, out
                 add_residual(ending)
             if not even and coming < PAIRS:
                 residual_term(coming)
+            if not even and n >= 3:
+                normalise_and_store(ending)

@@ -22,7 +22,7 @@ H_TILES = H // P
 K2_PASSES = H // (P * PACK)
 EPS = 1e-5
 
-VECTOR_COLS = 224
+VECTOR_COLS = 256
 RUN = 4
 
 TE_ROW, B2_ROW, G_ROW, B_ROW, B1_ROW = 0, 8, 32, 48, 64

@@ -22,13 +22,13 @@ H_TILES = H // P
 K2_PASSES = H // (P * PACK)
 EPS = 1e-5
 
-VECTOR_COLS = 256
+VECTOR_COLS = 224
 RUN = 4
 
 TE_ROW, B2_ROW, G_ROW, B_ROW, B1_ROW = 0, 8, 32, 48, 64
 
 PREFETCH = 4
-DRAIN = 2
+DRAIN = 3
 
 FLOPS = 2 * EXPERTS * SLOTS * D * H * 2
 
@@ -57,6 +57,7 @@ def tile_hdmodel_pb_kernel(tc, xs_mix, task_emb, W1, b1, W2, b2, ln_g, ln_b, out
         norm = ctx.enter_context(tc.tile_pool(name="norm", bufs=2))
         ps_one = ctx.enter_context(tc.psum_pool(name="ps_one", bufs=1))
         ps_two = ctx.enter_context(tc.psum_pool(name="ps_two", bufs=2))
+        ps_three = ctx.enter_context(tc.psum_pool(name="ps_three", bufs=3))
         ctx.enter_context(tc.manual_schedule())
 
         w_chunks = {}
@@ -188,13 +189,15 @@ def tile_hdmodel_pb_kernel(tc, xs_mix, task_emb, W1, b1, W2, b2, ln_g, ln_b, out
             nc.vector.tensor_tensor(out=resid[:], in0=pair_tiles[("teb2", i)][:], in1=x_all[:, i, :], op=ALU.add)
             pair_tiles[("resid", i)] = resid
 
-        def quantise_xs_and_spread_gain(i):
+        def quantise_xs(i):
             xs_codes = prep.tile([P, 2 * SLOTS], U32, align_bytes=64)
             xs_scales = prep.tile([P, 2 * SLOTS], U8, align_bytes=64)
             quantise(
                 nc, xs_codes[:], xs_scales[:], pair_tiles[("xs_grouped", i)][:].rearrange("q e b p t -> q (e b p t)")
             )
             xs_packed[i] = (xs_codes, xs_scales)
+
+        def spread_gain(i):
             gb_wide = prep.tile([P, 2 * (D // P), BATCH, PAIR_ROWS], BF16)
             nc.scalar.copy(
                 out=gb_wide[:],
@@ -203,7 +206,7 @@ def tile_hdmodel_pb_kernel(tc, xs_mix, task_emb, W1, b1, W2, b2, ln_g, ln_b, out
                 .unsqueeze(2)
                 .to_broadcast([P, 2 * (D // P), BATCH, PAIR_ROWS]),
             )
-            gb_ps = ps_two.tile([P, 2, D], BF16, tag="gb")
+            gb_ps = ps_three.tile([P, 2, D], BF16, tag="gb")
             for v in range(2):
                 for c in range(D // P):
                     nc.tensor.transpose(
@@ -215,7 +218,7 @@ def tile_hdmodel_pb_kernel(tc, xs_mix, task_emb, W1, b1, W2, b2, ln_g, ln_b, out
 
         def first_matmul(n, c):
             if c == 0:
-                h_tiles[("h_ps", n)] = ps_two.tile([P, H_TILES, SLOTS], F32, tag="h", name="h_ps")
+                h_tiles[("h_ps", n)] = ps_one.tile([P, H_TILES, SLOTS], F32, tag="h", name="h_ps")
             codes, scales = w_packed[(n, c)]
             xs_codes, xs_scales = xs_packed[n // 2]
             mine = slice((n % 2) * SLOTS, (n % 2 + 1) * SLOTS)
@@ -331,13 +334,13 @@ def tile_hdmodel_pb_kernel(tc, xs_mix, task_emb, W1, b1, W2, b2, ln_g, ln_b, out
         round_and_flip_xs(0)
         group_xs(0)
         residual_term(0)
-        quantise_xs_and_spread_gain(0)
+        quantise_xs(0)
 
         for n in range(EXPERTS + DRAIN):
             fresh = n < EXPERTS
             behind = 1 <= n <= EXPERTS
             even = n % 2 == 0
-            ending = n // 2 - 1
+            closing = (n - 3) // 2
             coming = (n + 1) // 2
 
             if n + PREFETCH < EXPERTS:
@@ -349,9 +352,9 @@ def tile_hdmodel_pb_kernel(tc, xs_mix, task_emb, W1, b1, W2, b2, ln_g, ln_b, out
             if behind:
                 add_bias(n - 1)
             if even and 2 <= n < EXPERTS:
-                quantise_xs_and_spread_gain(coming)
-            if not even and n >= 3:
-                variance(ending)
+                quantise_xs(coming)
+            if even and n >= 4:
+                centre_times_gain(closing)
 
             if behind:
                 quantise_chunk(n - 1, 3)
@@ -359,28 +362,30 @@ def tile_hdmodel_pb_kernel(tc, xs_mix, task_emb, W1, b1, W2, b2, ln_g, ln_b, out
                 regroup_chunk(n, 1)
             if behind:
                 silu(n - 1)
+            if even and fresh:
+                spread_gain(n // 2)
+            if not even and n >= 3:
+                add_residual(closing)
             if not even and coming < PAIRS:
                 round_and_flip_xs(coming)
 
             if fresh:
                 quantise_chunk(n, 0)
                 first_matmul(n, 0)
-            if behind:
-                second_matmul(n - 1)
-            if fresh:
                 regroup_chunk(n, 2)
-            if not even and n >= 3:
-                centre_times_gain(ending)
+            if even and n >= 4:
+                normalise_and_store(closing)
             if not even and coming < PAIRS:
                 group_xs(coming)
 
             if fresh:
                 quantise_chunk(n, 1)
                 first_matmul(n, 1)
+            if behind:
+                second_matmul(n - 1)
+            if fresh:
                 regroup_chunk(n, 3)
-            if even and n >= 2:
-                add_residual(ending)
             if not even and coming < PAIRS:
                 residual_term(coming)
             if not even and n >= 3:
-                normalise_and_store(ending)
+                variance(closing)

@@ -17,26 +17,27 @@ BATCH, EXPERTS, TASKS, D, H = 8, 16, 8, 512, 1024
 SLOTS = BATCH * TASKS
 PAIRS = EXPERTS // 2
 PAIR_ROWS = 2 * TASKS
-CHUNK = 512
 H_TILES = H // P
 K2_PASSES = H // (P * PACK)
 EPS = 1e-5
 
-VECTOR_COLS = 224
+COLS = 1024
+def vector_cols(n):
+    return 640 if n == 0 else 256 if n == EXPERTS - 1 else 432
+
 RUN = 4
 
 TE_ROW, B2_ROW, G_ROW, B_ROW, B1_ROW = 0, 8, 32, 48, 64
 
 PREFETCH = 4
-DRAIN = 3
 
 FLOPS = 2 * EXPERTS * SLOTS * D * H * 2
 
 
-def regroup(nc, grouped, rows):
+def regroup(nc, grouped, rows, vector_cols):
     dst = grouped.rearrange("p (c i) j -> p c j i", i=RUN)
     src = rows.rearrange("p j (c i) -> p c j i", i=RUN)
-    split = VECTOR_COLS // RUN
+    split = vector_cols // RUN
     nc.vector.tensor_copy(out=dst[:, :split], in_=src[:, :split])
     nc.scalar.copy(out=dst[:, split:], in_=src[:, split:])
 
@@ -49,71 +50,122 @@ def tile_hdmodel_pb_kernel(tc, xs_mix, task_emb, W1, b1, W2, b2, ln_g, ln_b, out
     nc = tc.nc
     with ExitStack() as ctx:
         const = ctx.enter_context(tc.tile_pool(name="const", bufs=1))
-        raw = ctx.enter_context(tc.tile_pool(name="raw", bufs=2 * (PREFETCH + 1)))
-        stage = ctx.enter_context(tc.tile_pool(name="stage", bufs=6))
-        wq = ctx.enter_context(tc.tile_pool(name="wq", bufs=8))
+        raw = ctx.enter_context(tc.tile_pool(name="raw", bufs=PREFETCH + 1))
+        stage = ctx.enter_context(tc.tile_pool(name="stage", bufs=2))
+        wq = ctx.enter_context(tc.tile_pool(name="wq", bufs=3))
         prep = ctx.enter_context(tc.tile_pool(name="prep", bufs=2))
         hid = ctx.enter_context(tc.tile_pool(name="hid", bufs=2))
         norm = ctx.enter_context(tc.tile_pool(name="norm", bufs=2))
         ps_one = ctx.enter_context(tc.psum_pool(name="ps_one", bufs=1))
         ps_two = ctx.enter_context(tc.psum_pool(name="ps_two", bufs=2))
-        ps_three = ctx.enter_context(tc.psum_pool(name="ps_three", bufs=3))
         ctx.enter_context(tc.manual_schedule())
 
-        w_chunks = {}
+        w_raw = {}
         w_grouped = {}
         w_packed = {}
         xs_packed = {}
         pair_tiles = {}
         h_tiles = {}
 
-        def load_weights(n):
-            w1_raw = raw.tile([P, PACK, H], BF16, tag="raw")
-            nc.sync.dma_start(out=w1_raw[:], in_=W1[n].rearrange("(p j) h -> p j h", j=PACK))
-            w2_raw = raw.tile([P, K2_PASSES, PACK, D], BF16, tag="raw")
+        def load_w1(n, half=None):
+            first, width = (0, COLS) if half is None else (half * COLS // 2, COLS // 2)
+            w1_raw = raw.tile([P, PACK, width], BF16, tag="raw1" if half is None else "raw1_half%d" % half)
             nc.sync.dma_start(
-                out=w2_raw[:].rearrange("p g t d -> p (g t) d"),
-                in_=W2[n].rearrange("(s p) d -> p s d", p=P),
+                out=w1_raw[:], in_=W1[n].rearrange("(p j) h -> p j h", j=PACK)[:, :, first : first + width]
             )
-            for c in range(H // CHUNK):
-                w_chunks[(n, c)] = w1_raw[:, :, c * CHUNK : (c + 1) * CHUNK]
+            w_raw.setdefault((1, n), []).append((first, width, w1_raw[:]))
+
+        def load_w2(n):
+            w2_raw = raw.tile([P, PACK, K2_PASSES, D], BF16, tag="raw2")
+            w2_rows = W2[n].rearrange("(g t p) d -> g p t d", g=K2_PASSES, p=P)
             for g in range(K2_PASSES):
-                w_chunks[(n, 2 + g)] = w2_raw[:, g]
+                nc.sync.dma_start(out=w2_raw[:, :, g, :], in_=w2_rows[g])
+            w_raw[(2, n)] = [(0, COLS, w2_raw[:].rearrange("p t g d -> p t (g d)"))]
 
-        def regroup_chunk(n, c):
-            g_tile = stage.tile([P, CHUNK, PACK], BF16, tag="grouped", align_bytes=64)
-            regroup(nc, g_tile[:], w_chunks[(n, c)])
-            w_grouped[(n, c)] = g_tile
+        def regroup_piece(layer, n, piece):
+            if piece == 0:
+                w_grouped[(layer, n)] = stage.tile(
+                    [P, COLS, PACK], BF16, tag="grouped%d" % layer, name="grouped", align_bytes=64
+                )
+            first, width, view = w_raw[(layer, n)][piece]
+            regroup(nc, w_grouped[(layer, n)][:, first : first + width], view, vector_cols(n) * width // COLS)
 
-        def quantise_chunk(n, c):
-            codes = wq.tile([P, CHUNK], U32, tag="codes", align_bytes=64)
-            scales = wq.tile([P, CHUNK], U8, tag="scales", align_bytes=64)
-            quantise(nc, codes[:], scales[:], w_grouped[(n, c)][:].rearrange("p w j -> p (w j)"))
-            w_packed[(n, c)] = (codes, scales)
+        def quantise_weight(layer, n):
+            codes = wq.tile([P, COLS], U32, tag="codes%d" % layer, align_bytes=64)
+            scales = wq.tile([P, COLS], U8, tag="scales%d" % layer, align_bytes=64)
+            quantise(nc, codes[:], scales[:], w_grouped[(layer, n)][:].rearrange("p w j -> p (w j)"))
+            w_packed[(layer, n)] = (codes, scales)
 
-        x_all = const.tile([P, PAIRS, D], BF16)
-        for b in range(BATCH):
-            nc.sync.dma_start(
-                out=x_all[b * PAIR_ROWS : (b + 1) * PAIR_ROWS, :, :],
-                in_=xs_mix[b].rearrange("(i e) p d -> (e p) i d", e=2),
-            )
-        for n in range(PREFETCH):
-            load_weights(n)
+        te_rows = const.tile([P, D], BF16)
+        nc.gpsimd.memset(te_rows[:], 0.0)
+        nc.sync.dma_start(out=te_rows[TE_ROW : TE_ROW + TASKS, :], in_=task_emb)
         vec_rows = const.tile([P, D], BF16)
         nc.vector.memset(vec_rows[:], 0.0)
-        nc.scalar.dma_start(out=vec_rows[TE_ROW : TE_ROW + TASKS, :], in_=task_emb)
-        nc.scalar.dma_start(out=vec_rows[B2_ROW : B2_ROW + EXPERTS, :], in_=b2)
-        nc.scalar.dma_start(out=vec_rows[G_ROW : G_ROW + EXPERTS, :], in_=ln_g)
-        nc.scalar.dma_start(out=vec_rows[B_ROW : B_ROW + EXPERTS, :], in_=ln_b)
-        nc.scalar.dma_start(
-            out=vec_rows[B1_ROW : B1_ROW + 2 * EXPERTS, :],
-            in_=b1.rearrange("n (g c) -> (n g) c", g=K2_PASSES),
-        )
-
         ident = const.tile([P, P], BF16)
         make_identity(nc, ident[:])
         neg_half = const.tile([P, 1], F32)
         nc.gpsimd.memset(neg_half[:], -0.5)
+
+        x_first = const.tile([P, D], BF16)
+        x_rest = const.tile([P, PAIRS - 1, D], BF16)
+
+        load_w1(0, 0)
+        for b in range(BATCH):
+            queue = nc.sync if b % 2 else nc.scalar
+            queue.dma_start(
+                out=x_first[b * PAIR_ROWS : (b + 1) * PAIR_ROWS, :],
+                in_=xs_mix[b, 0:2].rearrange("e p d -> (e p) d"),
+            )
+        load_w1(0, 1)
+        load_w2(0)
+        nc.sync.dma_start(out=vec_rows[TE_ROW : TE_ROW + TASKS, :], in_=task_emb)
+        nc.sync.dma_start(out=vec_rows[B2_ROW : B2_ROW + EXPERTS, :], in_=b2)
+        nc.sync.dma_start(out=vec_rows[G_ROW : G_ROW + EXPERTS, :], in_=ln_g)
+        nc.sync.dma_start(out=vec_rows[B_ROW : B_ROW + EXPERTS, :], in_=ln_b)
+        nc.sync.dma_start(
+            out=vec_rows[B1_ROW : B1_ROW + 2 * EXPERTS, :],
+            in_=b1.rearrange("n (g c) -> (n g) c", g=K2_PASSES),
+        )
+        load_w1(1)
+        table_probe = const.tile([P, 1], F32)
+        nc.scalar.activation(out=table_probe[:], in_=neg_half[:], func=ACT.Silu)
+
+        def load_x_rest(first, last):
+            for b in range(first, last):
+                nc.sync.dma_start(
+                    out=x_rest[b * PAIR_ROWS : (b + 1) * PAIR_ROWS, :, :],
+                    in_=xs_mix[b, 2:].rearrange("(i e) p d -> (e p) i d", e=2),
+                )
+
+        load_w2(1)
+        load_x_rest(0, 2)
+        load_w1(2)
+        load_x_rest(2, 5)
+        load_w2(2)
+        load_x_rest(5, BATCH)
+        for n in range(3, PREFETCH):
+            load_w1(n)
+            load_w2(n)
+
+        def x_of(i):
+            return x_first[:] if i == 0 else x_rest[:, i - 1, :]
+
+        sel_te = const.tile([P, BATCH, 2, TASKS], BF16)
+        nc.vector.tensor_copy(
+            out=sel_te[:].rearrange("q b e p -> q (b e) p"),
+            in_=ident[:, TE_ROW : TE_ROW + TASKS].unsqueeze(1).to_broadcast([P, BATCH * 2, TASKS]),
+        )
+        sel = const.tile([P, PAIRS, BATCH, 2, TASKS], BF16)
+        for i in range(PAIRS):
+            nc.vector.tensor_tensor(
+                out=sel[:, i],
+                in0=sel_te[:],
+                in1=ident[:, B2_ROW + 2 * i : B2_ROW + 2 * i + 2]
+                .unsqueeze(1)
+                .unsqueeze(3)
+                .to_broadcast([P, BATCH, 2, TASKS]),
+                op=ALU.add,
+            )
 
         h_grouped = []
         for e in range(2):
@@ -123,56 +175,49 @@ def tile_hdmodel_pb_kernel(tc, xs_mix, task_emb, W1, b1, W2, b2, ln_g, ln_b, out
             nc.vector.memset(h_tile[:], 0.0)
             h_grouped.append(h_tile)
 
-        vec_cols_ps = ps_one.tile([P, PACK, P], BF16, tag="flip")
-        for c in range(D // P):
-            nc.tensor.transpose(vec_cols_ps[:, c, :], vec_rows[:, c * P : (c + 1) * P], ident[:])
-        b1_col = const.tile([P, EXPERTS, K2_PASSES, PACK], F32)
-        nc.vector.tensor_copy(
-            out=b1_col[:],
-            in_=vec_cols_ps[:, :, B1_ROW : B1_ROW + 2 * EXPERTS].rearrange("q t (n g) -> q n g t", g=K2_PASSES),
-        )
-        gb_col = const.tile([P, 2, D // P, EXPERTS, TASKS], BF16)
-        for v in range(2):
-            first = G_ROW + v * EXPERTS
-            nc.vector.tensor_copy(
-                out=gb_col[:, v],
-                in_=vec_cols_ps[:, :, first : first + EXPERTS]
-                .unsqueeze(3)
-                .to_broadcast([P, D // P, EXPERTS, TASKS]),
-            )
-
-        sel_te = const.tile([P, BATCH, 2, TASKS], BF16)
-        nc.vector.tensor_copy(
-            out=sel_te[:].rearrange("q b e p -> q (b e) p"),
-            in_=ident[:, TE_ROW : TE_ROW + TASKS].unsqueeze(1).to_broadcast([P, BATCH * 2, TASKS]),
-        )
-        te_ps = ps_one.tile([P, D], F32, tag="spread")
-        nc.tensor.matmul(
-            te_ps[:], lhsT=sel_te[:].rearrange("q b e p -> q (b e p)"), rhs=vec_rows[:], start=True, stop=True
-        )
         te_rep = const.tile([P, D], BF16)
-        nc.scalar.copy(out=te_rep[:], in_=te_ps[:])
 
-        def round_and_flip_xs(i):
+        def spread_task_embedding():
+            te_ps = ps_one.tile([P, D], F32, tag="spread")
+            nc.tensor.matmul(
+                te_ps[:], lhsT=sel_te[:].rearrange("q b e p -> q (b e p)"), rhs=te_rows[:], start=True, stop=True
+            )
+            nc.vector.tensor_copy(out=te_rep[:], in_=te_ps[:])
+
+        b1_col = const.tile([P, EXPERTS, K2_PASSES, PACK], F32)
+        gb_col = const.tile([P, 2, D // P, EXPERTS, TASKS], BF16)
+
+        def turn_vectors():
+            vec_cols_ps = ps_one.tile([P, PACK, P], BF16, tag="flip")
+            for c in range(D // P):
+                nc.tensor.transpose(vec_cols_ps[:, c, :], vec_rows[:, c * P : (c + 1) * P], ident[:])
+            nc.vector.tensor_copy(
+                out=b1_col[:],
+                in_=vec_cols_ps[:, :, B1_ROW : B1_ROW + 2 * EXPERTS].rearrange("q t (n g) -> q n g t", g=K2_PASSES),
+            )
+            for v in range(2):
+                first = G_ROW + v * EXPERTS
+                nc.vector.tensor_copy(
+                    out=gb_col[:, v],
+                    in_=vec_cols_ps[:, :, first : first + EXPERTS]
+                    .unsqueeze(3)
+                    .to_broadcast([P, D // P, EXPERTS, TASKS]),
+                )
+
+        def round_xs(i):
             xs16 = prep.tile([P, D], BF16)
-            nc.vector.tensor_tensor(out=xs16[:], in0=x_all[:, i, :], in1=te_rep[:], op=ALU.add)
+            nc.vector.tensor_tensor(out=xs16[:], in0=x_of(i), in1=te_rep[:], op=ALU.add)
+            pair_tiles[("xs16", i)] = xs16
+
+        def flip_xs(i):
+            xs16 = pair_tiles[("xs16", i)]
             xs_flip = ps_one.tile([P, PACK, P], BF16, tag="flip")
             xs16_by_t = xs16[:].rearrange("r (q t) -> r t q", t=PACK)
             for t in range(PACK):
                 nc.tensor.transpose(xs_flip[:, t, :], xs16_by_t[:, t, :], ident[:])
-            sel = prep.tile([P, BATCH, 2, TASKS], BF16)
-            nc.vector.tensor_tensor(
-                out=sel[:],
-                in0=sel_te[:],
-                in1=ident[:, B2_ROW + 2 * i : B2_ROW + 2 * i + 2]
-                .unsqueeze(1)
-                .unsqueeze(3)
-                .to_broadcast([P, BATCH, 2, TASKS]),
-                op=ALU.add,
-            )
             teb2_ps = ps_one.tile([P, D], F32, tag="spread")
             nc.tensor.matmul(
-                teb2_ps[:], lhsT=sel[:].rearrange("q b e p -> q (b e p)"), rhs=vec_rows[:], start=True, stop=True
+                teb2_ps[:], lhsT=sel[:, i].rearrange("q b e p -> q (b e p)"), rhs=vec_rows[:], start=True, stop=True
             )
             pair_tiles[("xs_flip", i)] = xs_flip
             pair_tiles[("teb2", i)] = teb2_ps
@@ -186,7 +231,7 @@ def tile_hdmodel_pb_kernel(tc, xs_mix, task_emb, W1, b1, W2, b2, ln_g, ln_b, out
 
         def residual_term(i):
             resid = prep.tile([P, D], F32)
-            nc.vector.tensor_tensor(out=resid[:], in0=pair_tiles[("teb2", i)][:], in1=x_all[:, i, :], op=ALU.add)
+            nc.vector.tensor_tensor(out=resid[:], in0=pair_tiles[("teb2", i)][:], in1=x_of(i), op=ALU.add)
             pair_tiles[("resid", i)] = resid
 
         def quantise_xs(i):
@@ -206,7 +251,11 @@ def tile_hdmodel_pb_kernel(tc, xs_mix, task_emb, W1, b1, W2, b2, ln_g, ln_b, out
                 .unsqueeze(2)
                 .to_broadcast([P, 2 * (D // P), BATCH, PAIR_ROWS]),
             )
-            gb_ps = ps_three.tile([P, 2, D], BF16, tag="gb")
+            pair_tiles[("gb_wide", i)] = gb_wide
+
+        def flip_gain(i):
+            gb_wide = pair_tiles[("gb_wide", i)]
+            gb_ps = ps_two.tile([P, 2, D], BF16, tag="gb")
             for v in range(2):
                 for c in range(D // P):
                     nc.tensor.transpose(
@@ -216,15 +265,14 @@ def tile_hdmodel_pb_kernel(tc, xs_mix, task_emb, W1, b1, W2, b2, ln_g, ln_b, out
                     )
             pair_tiles[("gb", i)] = gb_ps
 
-        def first_matmul(n, c):
-            if c == 0:
-                h_tiles[("h_ps", n)] = ps_one.tile([P, H_TILES, SLOTS], F32, tag="h", name="h_ps")
-            codes, scales = w_packed[(n, c)]
+        def first_matmul(n):
+            h_tiles[("h_ps", n)] = ps_two.tile([P, H_TILES, SLOTS], F32, tag="h", name="h_ps")
+            codes, scales = w_packed[(1, n)]
             xs_codes, xs_scales = xs_packed[n // 2]
             mine = slice((n % 2) * SLOTS, (n % 2 + 1) * SLOTS)
-            for m in range(CHUNK // P):
+            for m in range(H_TILES):
                 nc.tensor.matmul_mx(
-                    out=h_tiles[("h_ps", n)][:, c * (CHUNK // P) + m, :],
+                    out=h_tiles[("h_ps", n)][:, m, :],
                     lhsT=codes[:, m * P : (m + 1) * P].bitcast(FP8X4),
                     lhsT_scale=scales[:, m * P : (m + 1) * P],
                     rhs=xs_codes[:, mine].bitcast(FP8X4),
@@ -255,13 +303,14 @@ def tile_hdmodel_pb_kernel(tc, xs_mix, task_emb, W1, b1, W2, b2, ln_g, ln_b, out
             if e == 0:
                 pair_tiles[("mlp", i)] = ps_two.tile([P, D], F32, tag="mlp", name="mlp_ps")
             for g in range(K2_PASSES):
-                codes, scales = w_packed[(n, 2 + g)]
+                codes, scales = w_packed[(2, n)]
+                mine = slice(g * D, (g + 1) * D)
                 nc.tensor.matmul_mx(
                     out=pair_tiles[("mlp", i)][:],
                     lhsT=h_codes[:, g * P : (g + 1) * P].bitcast(FP8X4),
                     lhsT_scale=h_scales[:, g * P : (g + 1) * P],
-                    rhs=codes[:].bitcast(FP8X4),
-                    rhs_scale=scales[:],
+                    rhs=codes[:, mine].bitcast(FP8X4),
+                    rhs_scale=scales[:, mine],
                     start=(e == 0 and g == 0),
                     stop=(e == 1 and g == K2_PASSES - 1),
                 )
@@ -331,61 +380,74 @@ def tile_hdmodel_pb_kernel(tc, xs_mix, task_emb, W1, b1, W2, b2, ln_g, ln_b, out
                     in_=y[b * PAIR_ROWS : (b + 1) * PAIR_ROWS, :],
                 )
 
-        round_and_flip_xs(0)
-        group_xs(0)
-        residual_term(0)
-        quantise_xs(0)
-
-        for n in range(EXPERTS + DRAIN):
-            fresh = n < EXPERTS
-            behind = 1 <= n <= EXPERTS
+        for n in range(EXPERTS):
             even = n % 2 == 0
-            closing = (n - 3) // 2
-            coming = (n + 1) // 2
-
             if n + PREFETCH < EXPERTS:
-                load_weights(n + PREFETCH)
-            if behind:
-                quantise_chunk(n - 1, 2)
-            if fresh:
-                regroup_chunk(n, 0)
-            if behind:
+                load_w1(n + PREFETCH)
+                load_w2(n + PREFETCH)
+
+            regroup_piece(1, n, 0)
+            if n == 0:
+                spread_task_embedding()
+                round_xs(0)
+                flip_xs(0)
+                regroup_piece(1, 0, 1)
+            if n >= 1:
+                if not even:
+                    quantise_xs(n // 2)
+                quantise_weight(1, n - 1)
+                first_matmul(n - 1)
+            if even and n >= 2:
+                flip_xs(n // 2)
+            if even and n >= 4:
+                flip_gain(n // 2 - 2)
+            if n >= 2:
+                silu(n - 2)
+            regroup_piece(2, n, 0)
+
+            if even and n >= 4:
+                add_residual(n // 2 - 2)
+            if not even and n >= 5:
+                centre_times_gain(n // 2 - 2)
+            if n == 1 or even and n >= 2:
+                residual_term(n // 2)
+            if n >= 1:
                 add_bias(n - 1)
-            if even and 2 <= n < EXPERTS:
-                quantise_xs(coming)
+            if not even and n >= 5:
+                normalise_and_store(n // 2 - 2)
+
+            if n >= 1:
+                quantise_weight(2, n - 1)
+            if n >= 2:
+                second_matmul(n - 2)
+            if even:
+                group_xs(n // 2)
+            if n == 0:
+                turn_vectors()
+            if not even and n + 1 < EXPERTS:
+                round_xs(n // 2 + 1)
             if even and n >= 4:
-                centre_times_gain(closing)
-
-            if behind:
-                quantise_chunk(n - 1, 3)
-            if fresh:
-                regroup_chunk(n, 1)
-            if behind:
-                silu(n - 1)
-            if even and fresh:
-                spread_gain(n // 2)
+                variance(n // 2 - 2)
             if not even and n >= 3:
-                add_residual(closing)
-            if not even and coming < PAIRS:
-                round_and_flip_xs(coming)
+                spread_gain(n // 2 - 1)
 
-            if fresh:
-                quantise_chunk(n, 0)
-                first_matmul(n, 0)
-                regroup_chunk(n, 2)
-            if even and n >= 4:
-                normalise_and_store(closing)
-            if not even and coming < PAIRS:
-                group_xs(coming)
-
-            if fresh:
-                quantise_chunk(n, 1)
-                first_matmul(n, 1)
-            if behind:
-                second_matmul(n - 1)
-            if fresh:
-                regroup_chunk(n, 3)
-            if not even and coming < PAIRS:
-                residual_term(coming)
-            if not even and n >= 3:
-                variance(closing)
+        last = EXPERTS - 1
+        silu(last - 1)
+        quantise_weight(1, last)
+        first_matmul(last)
+        second_matmul(last - 1)
+        flip_gain(PAIRS - 2)
+        add_residual(PAIRS - 2)
+        add_bias(last)
+        silu(last)
+        variance(PAIRS - 2)
+        spread_gain(PAIRS - 1)
+        quantise_weight(2, last)
+        second_matmul(last)
+        flip_gain(PAIRS - 1)
+        centre_times_gain(PAIRS - 2)
+        normalise_and_store(PAIRS - 2)
+        add_residual(PAIRS - 1)
+        variance(PAIRS - 1)
+        centre_times_gain(PAIRS - 1)
+        normalise_and_store(PAIRS - 1)

@@ -23,8 +23,9 @@ EPS = 1e-5
 
 COLS = 1024
 def vector_cols(n):
-    return 640 if n == 0 else 256 if n == EXPERTS - 1 else 432
+    return 640 if n == 0 else 256 if n == EXPERTS - 1 else 352
 
+GPSIMD_COLS = 224
 RUN = 4
 
 TE_ROW, B2_ROW, G_ROW, B_ROW, B1_ROW = 0, 8, 32, 48, 64
@@ -34,12 +35,21 @@ PREFETCH = 4
 FLOPS = 2 * EXPERTS * SLOTS * D * H * 2
 
 
-def regroup(nc, grouped, rows, vector_cols):
+def gpsimd_cols(n):
+    return GPSIMD_COLS if 1 <= n < EXPERTS else 0
+
+
+def regroup(nc, grouped, rows, vector_cols, gpsimd_cols):
     dst = grouped.rearrange("p (c i) j -> p c j i", i=RUN)
     src = rows.rearrange("p j (c i) -> p c j i", i=RUN)
-    split = vector_cols // RUN
-    nc.vector.tensor_copy(out=dst[:, :split], in_=src[:, :split])
-    nc.scalar.copy(out=dst[:, split:], in_=src[:, split:])
+    a = vector_cols // RUN
+    b = a + gpsimd_cols // RUN
+    nc.vector.tensor_copy(out=dst[:, :a], in_=src[:, :a])
+    if gpsimd_cols:
+        nc.gpsimd.tensor_scalar(
+            out=dst[:, a - 1 : b], in0=src[:, a - 1 : b], scalar1=1.0, scalar2=0.0, op0=ALU.mult, op1=ALU.add
+        )
+    nc.scalar.copy(out=dst[:, b:], in_=src[:, b:])
 
 
 def quantise(nc, codes, scales, grouped):
@@ -80,7 +90,10 @@ def tile_hdmodel_pb_kernel(tc, xs_mix, task_emb, W1, b1, W2, b2, ln_g, ln_b, out
             w2_rows = W2[n].rearrange("(g t p) d -> g p t d", g=K2_PASSES, p=P)
             for g in range(K2_PASSES):
                 nc.sync.dma_start(out=w2_raw[:, :, g, :], in_=w2_rows[g])
-            w_raw[(2, n)] = [(0, COLS, w2_raw[:].rearrange("p t g d -> p t (g d)"))]
+            if n == 0:
+                w_raw[(2, n)] = [(g * D, D, w2_raw[:, :, g, :]) for g in range(K2_PASSES)]
+            else:
+                w_raw[(2, n)] = [(0, COLS, w2_raw[:].rearrange("p t g d -> p t (g d)"))]
 
         def regroup_piece(layer, n, piece):
             if piece == 0:
@@ -88,7 +101,7 @@ def tile_hdmodel_pb_kernel(tc, xs_mix, task_emb, W1, b1, W2, b2, ln_g, ln_b, out
                     [P, COLS, PACK], BF16, tag="grouped%d" % layer, name="grouped", align_bytes=64
                 )
             first, width, view = w_raw[(layer, n)][piece]
-            regroup(nc, w_grouped[(layer, n)][:, first : first + width], view, vector_cols(n) * width // COLS)
+            regroup(nc, w_grouped[(layer, n)][:, first : first + width], view, vector_cols(n) * width // COLS, gpsimd_cols(n) if layer == 2 else 0)
 
         def quantise_weight(layer, n):
             codes = wq.tile([P, COLS], U32, tag="codes%d" % layer, align_bytes=64)
@@ -116,16 +129,16 @@ def tile_hdmodel_pb_kernel(tc, xs_mix, task_emb, W1, b1, W2, b2, ln_g, ln_b, out
                 out=x_first[b * PAIR_ROWS : (b + 1) * PAIR_ROWS, :],
                 in_=xs_mix[b, 0:2].rearrange("e p d -> (e p) d"),
             )
-        load_w1(0, 1)
-        load_w2(0)
-        nc.sync.dma_start(out=vec_rows[TE_ROW : TE_ROW + TASKS, :], in_=task_emb)
-        nc.sync.dma_start(out=vec_rows[B2_ROW : B2_ROW + EXPERTS, :], in_=b2)
-        nc.sync.dma_start(out=vec_rows[G_ROW : G_ROW + EXPERTS, :], in_=ln_g)
-        nc.sync.dma_start(out=vec_rows[B_ROW : B_ROW + EXPERTS, :], in_=ln_b)
+        nc.scalar.dma_start(out=vec_rows[TE_ROW : TE_ROW + TASKS, :], in_=task_emb)
+        nc.scalar.dma_start(out=vec_rows[B2_ROW : B2_ROW + EXPERTS, :], in_=b2)
+        nc.scalar.dma_start(out=vec_rows[G_ROW : G_ROW + EXPERTS, :], in_=ln_g)
+        nc.scalar.dma_start(out=vec_rows[B_ROW : B_ROW + EXPERTS, :], in_=ln_b)
         nc.sync.dma_start(
             out=vec_rows[B1_ROW : B1_ROW + 2 * EXPERTS, :],
             in_=b1.rearrange("n (g c) -> (n g) c", g=K2_PASSES),
         )
+        load_w1(0, 1)
+        load_w2(0)
         load_w1(1)
         table_probe = const.tile([P, 1], F32)
         nc.scalar.activation(out=table_probe[:], in_=neg_half[:], func=ACT.Silu)
@@ -188,7 +201,7 @@ def tile_hdmodel_pb_kernel(tc, xs_mix, task_emb, W1, b1, W2, b2, ln_g, ln_b, out
         gb_col = const.tile([P, 2, D // P, EXPERTS, TASKS], BF16)
 
         def turn_vectors():
-            vec_cols_ps = ps_one.tile([P, PACK, P], BF16, tag="flip")
+            vec_cols_ps = ps_two.tile([P, PACK, P], BF16, tag="gb")
             for c in range(D // P):
                 nc.tensor.transpose(vec_cols_ps[:, c, :], vec_rows[:, c * P : (c + 1) * P], ident[:])
             nc.vector.tensor_copy(
@@ -392,6 +405,8 @@ def tile_hdmodel_pb_kernel(tc, xs_mix, task_emb, W1, b1, W2, b2, ln_g, ln_b, out
                 round_xs(0)
                 flip_xs(0)
                 regroup_piece(1, 0, 1)
+                group_xs(0)
+                turn_vectors()
             if n >= 1:
                 if not even:
                     quantise_xs(n // 2)
@@ -404,6 +419,8 @@ def tile_hdmodel_pb_kernel(tc, xs_mix, task_emb, W1, b1, W2, b2, ln_g, ln_b, out
             if n >= 2:
                 silu(n - 2)
             regroup_piece(2, n, 0)
+            if n == 0:
+                regroup_piece(2, 0, 1)
 
             if even and n >= 4:
                 add_residual(n // 2 - 2)
@@ -420,10 +437,8 @@ def tile_hdmodel_pb_kernel(tc, xs_mix, task_emb, W1, b1, W2, b2, ln_g, ln_b, out
                 quantise_weight(2, n - 1)
             if n >= 2:
                 second_matmul(n - 2)
-            if even:
+            if even and n >= 2:
                 group_xs(n // 2)
-            if n == 0:
-                turn_vectors()
             if not even and n + 1 < EXPERTS:
                 round_xs(n // 2 + 1)
             if even and n >= 4:

@@ -26,10 +26,11 @@ def vector_cols(n):
     return 640 if n == 0 else 256 if n == EXPERTS - 1 else 352
 
 GPSIMD_COLS = 224
-RUN = 4
+RUN = 2
 
 TE_ROW, B2_ROW, G_ROW, B_ROW, B1_ROW = 0, 8, 32, 48, 64
 
+FIRST_PAIRS = 2
 PREFETCH = 4
 
 FLOPS = 2 * EXPERTS * SLOTS * D * H * 2
@@ -46,8 +47,14 @@ def regroup(nc, grouped, rows, vector_cols, gpsimd_cols):
     b = a + gpsimd_cols // RUN
     nc.vector.tensor_copy(out=dst[:, :a], in_=src[:, :a])
     if gpsimd_cols:
+        mine = slice((a - 1) * RUN, b * RUN)
         nc.gpsimd.tensor_scalar(
-            out=dst[:, a - 1 : b], in0=src[:, a - 1 : b], scalar1=1.0, scalar2=0.0, op0=ALU.mult, op1=ALU.add
+            out=grouped[:, mine, :],
+            in0=rows[:, :, mine].rearrange("p j w -> p w j"),
+            scalar1=1.0,
+            scalar2=0.0,
+            op0=ALU.mult,
+            op1=ALU.add,
         )
     nc.scalar.copy(out=dst[:, b:], in_=src[:, b:])
 
@@ -119,15 +126,15 @@ def tile_hdmodel_pb_kernel(tc, xs_mix, task_emb, W1, b1, W2, b2, ln_g, ln_b, out
         neg_half = const.tile([P, 1], F32)
         nc.gpsimd.memset(neg_half[:], -0.5)
 
-        x_first = const.tile([P, D], BF16)
-        x_rest = const.tile([P, PAIRS - 1, D], BF16)
+        x_first = const.tile([P, FIRST_PAIRS, D], BF16)
+        x_rest = const.tile([P, PAIRS - FIRST_PAIRS, D], BF16)
 
         load_w1(0, 0)
         for b in range(BATCH):
             queue = nc.sync if b % 2 else nc.scalar
             queue.dma_start(
-                out=x_first[b * PAIR_ROWS : (b + 1) * PAIR_ROWS, :],
-                in_=xs_mix[b, 0:2].rearrange("e p d -> (e p) d"),
+                out=x_first[b * PAIR_ROWS : (b + 1) * PAIR_ROWS, :, :],
+                in_=xs_mix[b, : 2 * FIRST_PAIRS].rearrange("(i e) p d -> (e p) i d", e=2),
             )
         nc.scalar.dma_start(out=vec_rows[TE_ROW : TE_ROW + TASKS, :], in_=task_emb)
         nc.scalar.dma_start(out=vec_rows[B2_ROW : B2_ROW + EXPERTS, :], in_=b2)
@@ -147,7 +154,7 @@ def tile_hdmodel_pb_kernel(tc, xs_mix, task_emb, W1, b1, W2, b2, ln_g, ln_b, out
             for b in range(first, last):
                 nc.sync.dma_start(
                     out=x_rest[b * PAIR_ROWS : (b + 1) * PAIR_ROWS, :, :],
-                    in_=xs_mix[b, 2:].rearrange("(i e) p d -> (e p) i d", e=2),
+                    in_=xs_mix[b, 2 * FIRST_PAIRS :].rearrange("(i e) p d -> (e p) i d", e=2),
                 )
 
         load_w2(1)
@@ -161,7 +168,7 @@ def tile_hdmodel_pb_kernel(tc, xs_mix, task_emb, W1, b1, W2, b2, ln_g, ln_b, out
             load_w2(n)
 
         def x_of(i):
-            return x_first[:] if i == 0 else x_rest[:, i - 1, :]
+            return x_first[:, i, :] if i < FIRST_PAIRS else x_rest[:, i - FIRST_PAIRS, :]
 
         sel_te = const.tile([P, BATCH, 2, TASKS], BF16)
         nc.vector.tensor_copy(

@@ -22,8 +22,12 @@ K2_PASSES = H // (P * PACK)
 EPS = 1e-5
 
 COLS = 1024
-def vector_cols(n):
-    return 640 if n == 0 else 256 if n == EXPERTS - 1 else 352
+def vector_cols(layer, n):
+    if n == 0:
+        return 640
+    if n == EXPERTS - 1:
+        return 256 if layer == 2 else 176
+    return 256 if layer == 1 and n >= 2 else 464
 
 GPSIMD_COLS = 224
 RUN = 2
@@ -36,27 +40,22 @@ PREFETCH = 4
 FLOPS = 2 * EXPERTS * SLOTS * D * H * 2
 
 
-def gpsimd_cols(n):
-    return GPSIMD_COLS if 1 <= n < EXPERTS else 0
+def gpsimd_cols(layer, n):
+    return GPSIMD_COLS if layer == 1 and n >= 2 else 0
 
 
-def regroup(nc, grouped, rows, vector_cols, gpsimd_cols):
+def regroup(nc, grouped, rows, vector_end, scalar_first):
     dst = grouped.rearrange("p (c i) j -> p c j i", i=RUN)
     src = rows.rearrange("p j (c i) -> p c j i", i=RUN)
-    a = vector_cols // RUN
-    b = a + gpsimd_cols // RUN
+    a, b = vector_end // RUN, scalar_first // RUN
     nc.vector.tensor_copy(out=dst[:, :a], in_=src[:, :a])
-    if gpsimd_cols:
-        mine = slice((a - 1) * RUN, b * RUN)
-        nc.gpsimd.tensor_scalar(
-            out=grouped[:, mine, :],
-            in0=rows[:, :, mine].rearrange("p j w -> p w j"),
-            scalar1=1.0,
-            scalar2=0.0,
-            op0=ALU.mult,
-            op1=ALU.add,
-        )
     nc.scalar.copy(out=dst[:, b:], in_=src[:, b:])
+
+
+def regroup_on_gpsimd(nc, grouped, rows):
+    nc.gpsimd.tensor_scalar(
+        out=grouped, in0=rows.rearrange("p j w -> p w j"), scalar1=1.0, scalar2=0.0, op0=ALU.mult, op1=ALU.add
+    )
 
 
 def quantise(nc, codes, scales, grouped):
@@ -70,7 +69,7 @@ def tile_hdmodel_pb_kernel(tc, xs_mix, task_emb, W1, b1, W2, b2, ln_g, ln_b, out
         raw = ctx.enter_context(tc.tile_pool(name="raw", bufs=PREFETCH + 1))
         stage = ctx.enter_context(tc.tile_pool(name="stage", bufs=2))
         wq = ctx.enter_context(tc.tile_pool(name="wq", bufs=3))
-        prep = ctx.enter_context(tc.tile_pool(name="prep", bufs=2))
+        prep = ctx.enter_context(tc.tile_pool(name="prep", bufs=3))
         hid = ctx.enter_context(tc.tile_pool(name="hid", bufs=2))
         norm = ctx.enter_context(tc.tile_pool(name="norm", bufs=2))
         ps_one = ctx.enter_context(tc.psum_pool(name="ps_one", bufs=1))
@@ -86,7 +85,10 @@ def tile_hdmodel_pb_kernel(tc, xs_mix, task_emb, W1, b1, W2, b2, ln_g, ln_b, out
 
         def load_w1(n, half=None):
             first, width = (0, COLS) if half is None else (half * COLS // 2, COLS // 2)
-            w1_raw = raw.tile([P, PACK, width], BF16, tag="raw1" if half is None else "raw1_half%d" % half)
+            if half is None:
+                w1_raw = raw.tile([P, PACK, width], BF16, tag="raw1")
+            else:
+                w1_raw = const.tile([P, PACK, width], BF16, name="raw1_half%d" % half)
             nc.sync.dma_start(
                 out=w1_raw[:], in_=W1[n].rearrange("(p j) h -> p j h", j=PACK)[:, :, first : first + width]
             )
@@ -102,13 +104,30 @@ def tile_hdmodel_pb_kernel(tc, xs_mix, task_emb, W1, b1, W2, b2, ln_g, ln_b, out
             else:
                 w_raw[(2, n)] = [(0, COLS, w2_raw[:].rearrange("p t g d -> p t (g d)"))]
 
+        def new_grouped(layer, n):
+            w_grouped[(layer, n)] = stage.tile(
+                [P, COLS, PACK], BF16, tag="grouped%d" % layer, name="grouped", align_bytes=64
+            )
+
+        def gpsimd_share(layer, n):
+            new_grouped(layer, n)
+            first = vector_cols(layer, n)
+            mine = slice(first, first + gpsimd_cols(layer, n))
+            ((start, width, view),) = w_raw[(layer, n)]
+            regroup_on_gpsimd(nc, w_grouped[(layer, n)][:, mine, :], view[:, :, mine])
+
         def regroup_piece(layer, n, piece):
-            if piece == 0:
-                w_grouped[(layer, n)] = stage.tile(
-                    [P, COLS, PACK], BF16, tag="grouped%d" % layer, name="grouped", align_bytes=64
-                )
+            if (layer, n) not in w_grouped:
+                new_grouped(layer, n)
             first, width, view = w_raw[(layer, n)][piece]
-            regroup(nc, w_grouped[(layer, n)][:, first : first + width], view, vector_cols(n) * width // COLS, gpsimd_cols(n) if layer == 2 else 0)
+            vector_end = vector_cols(layer, n) * width // COLS
+            regroup(
+                nc,
+                w_grouped[(layer, n)][:, first : first + width],
+                view,
+                vector_end,
+                vector_end + gpsimd_cols(layer, n),
+            )
 
         def quantise_weight(layer, n):
             codes = wq.tile([P, COLS], U32, tag="codes%d" % layer, align_bytes=64)
@@ -145,8 +164,8 @@ def tile_hdmodel_pb_kernel(tc, xs_mix, task_emb, W1, b1, W2, b2, ln_g, ln_b, out
             in_=b1.rearrange("n (g c) -> (n g) c", g=K2_PASSES),
         )
         load_w1(0, 1)
-        load_w2(0)
         load_w1(1)
+        load_w2(0)
         table_probe = const.tile([P, 1], F32)
         nc.scalar.activation(out=table_probe[:], in_=neg_half[:], func=ACT.Silu)
 
@@ -157,15 +176,15 @@ def tile_hdmodel_pb_kernel(tc, xs_mix, task_emb, W1, b1, W2, b2, ln_g, ln_b, out
                     in_=xs_mix[b, 2 * FIRST_PAIRS :].rearrange("(i e) p d -> (e p) i d", e=2),
                 )
 
-        load_w2(1)
-        load_x_rest(0, 2)
         load_w1(2)
+        load_x_rest(0, 2)
+        load_w2(1)
         load_x_rest(2, 5)
-        load_w2(2)
+        load_w1(3)
         load_x_rest(5, BATCH)
-        for n in range(3, PREFETCH):
-            load_w1(n)
-            load_w2(n)
+        load_w2(2)
+        load_w1(4)
+        load_w2(3)
 
         def x_of(i):
             return x_first[:, i, :] if i < FIRST_PAIRS else x_rest[:, i - FIRST_PAIRS, :]
@@ -400,76 +419,70 @@ def tile_hdmodel_pb_kernel(tc, xs_mix, task_emb, W1, b1, W2, b2, ln_g, ln_b, out
                     in_=y[b * PAIR_ROWS : (b + 1) * PAIR_ROWS, :],
                 )
 
+        regroup_piece(1, 0, 0)
+        spread_task_embedding()
+        round_xs(0)
+        flip_xs(0)
+        regroup_piece(1, 0, 1)
+        group_xs(0)
+        turn_vectors()
         for n in range(EXPERTS):
             even = n % 2 == 0
+            if n + PREFETCH + 1 < EXPERTS:
+                load_w1(n + PREFETCH + 1)
             if n + PREFETCH < EXPERTS:
-                load_w1(n + PREFETCH)
                 load_w2(n + PREFETCH)
 
-            regroup_piece(1, n, 0)
-            if n == 0:
-                spread_task_embedding()
-                round_xs(0)
-                flip_xs(0)
-                regroup_piece(1, 0, 1)
-                group_xs(0)
-                turn_vectors()
+            if n + 1 < EXPERTS:
+                regroup_piece(1, n + 1, 0)
+            if even:
+                quantise_xs(n // 2)
+            quantise_weight(1, n)
+            first_matmul(n)
+            if n + 2 < EXPERTS:
+                gpsimd_share(1, n + 2)
+            if not even and n + 1 < EXPERTS:
+                flip_xs(n // 2 + 1)
+            if not even and n >= 3:
+                flip_gain(n // 2 - 1)
             if n >= 1:
-                if not even:
-                    quantise_xs(n // 2)
-                quantise_weight(1, n - 1)
-                first_matmul(n - 1)
-            if even and n >= 2:
-                flip_xs(n // 2)
-            if even and n >= 4:
-                flip_gain(n // 2 - 2)
-            if n >= 2:
-                silu(n - 2)
-            regroup_piece(2, n, 0)
-            if n == 0:
-                regroup_piece(2, 0, 1)
+                silu(n - 1)
+            for piece in range(len(w_raw[(2, n)])):
+                regroup_piece(2, n, piece)
 
+            if not even and n >= 3:
+                add_residual(n // 2 - 1)
             if even and n >= 4:
-                add_residual(n // 2 - 2)
-            if not even and n >= 5:
                 centre_times_gain(n // 2 - 2)
-            if n == 1 or even and n >= 2:
-                residual_term(n // 2)
-            if n >= 1:
-                add_bias(n - 1)
-            if not even and n >= 5:
+            if n == 0:
+                residual_term(0)
+            if not even and n + 1 < EXPERTS:
+                residual_term(n // 2 + 1)
+            add_bias(n)
+            if even and n >= 4:
                 normalise_and_store(n // 2 - 2)
 
             if n >= 1:
                 quantise_weight(2, n - 1)
-            if n >= 2:
-                second_matmul(n - 2)
-            if even and n >= 2:
-                group_xs(n // 2)
-            if not even and n + 1 < EXPERTS:
+                second_matmul(n - 1)
+            if even and n + 2 < EXPERTS:
                 round_xs(n // 2 + 1)
-            if even and n >= 4:
-                variance(n // 2 - 2)
+            if not even and n + 1 < EXPERTS:
+                group_xs(n // 2 + 1)
             if not even and n >= 3:
+                variance(n // 2 - 1)
+            if even and n >= 2:
                 spread_gain(n // 2 - 1)
 
         last = EXPERTS - 1
-        silu(last - 1)
-        quantise_weight(1, last)
-        first_matmul(last)
-        second_matmul(last - 1)
-        flip_gain(PAIRS - 2)
-        add_residual(PAIRS - 2)
-        add_bias(last)
         silu(last)
-        variance(PAIRS - 2)
         spread_gain(PAIRS - 1)
         quantise_weight(2, last)
         second_matmul(last)
         flip_gain(PAIRS - 1)
         centre_times_gain(PAIRS - 2)
-        normalise_and_store(PAIRS - 2)
         add_residual(PAIRS - 1)
         variance(PAIRS - 1)
+        normalise_and_store(PAIRS - 2)
         centre_times_gain(PAIRS - 1)
         normalise_and_store(PAIRS - 1)

@@ -16,7 +16,6 @@ PACK = 4
 BATCH, EXPERTS, TASKS, D, H = 8, 16, 8, 512, 1024
 SLOTS = BATCH * TASKS
 PAIRS = EXPERTS // 2
-PAIR_ROWS = 2 * TASKS
 H_TILES = H // P
 K2_PASSES = H // (P * PACK)
 EPS = 1e-5
@@ -34,7 +33,6 @@ RUN = 2
 
 TE_ROW, B2_ROW, G_ROW, B_ROW, B1_ROW = 0, 8, 32, 48, 64
 
-FIRST_PAIRS = 2
 PREFETCH = 4
 
 FLOPS = 2 * EXPERTS * SLOTS * D * H * 2
@@ -145,81 +143,69 @@ def tile_hdmodel_pb_kernel(tc, xs_mix, task_emb, W1, b1, W2, b2, ln_g, ln_b, out
         neg_half = const.tile([P, 1], F32)
         nc.gpsimd.memset(neg_half[:], -0.5)
 
-        x_first = const.tile([P, FIRST_PAIRS, D], BF16)
-        x_rest = const.tile([P, PAIRS - FIRST_PAIRS, D], BF16)
+        x_all = const.tile([P, PAIRS, D], BF16)
+
+        def load_xs(queue, i):
+            for e in range(2):
+                queue.dma_start(out=x_all[e * SLOTS : (e + 1) * SLOTS, i, :], in_=xs_mix[:, 2 * i + e])
 
         load_w1(0, 0)
-        for b in range(BATCH):
-            queue = nc.sync if b % 2 else nc.scalar
-            queue.dma_start(
-                out=x_first[b * PAIR_ROWS : (b + 1) * PAIR_ROWS, :, :],
-                in_=xs_mix[b, : 2 * FIRST_PAIRS].rearrange("(i e) p d -> (e p) i d", e=2),
-            )
+        load_xs(nc.scalar, 0)
         nc.scalar.dma_start(out=vec_rows[TE_ROW : TE_ROW + TASKS, :], in_=task_emb)
         nc.scalar.dma_start(out=vec_rows[B2_ROW : B2_ROW + EXPERTS, :], in_=b2)
         nc.scalar.dma_start(out=vec_rows[G_ROW : G_ROW + EXPERTS, :], in_=ln_g)
         nc.scalar.dma_start(out=vec_rows[B_ROW : B_ROW + EXPERTS, :], in_=ln_b)
-        nc.sync.dma_start(
+        nc.scalar.dma_start(
             out=vec_rows[B1_ROW : B1_ROW + 2 * EXPERTS, :],
             in_=b1.rearrange("n (g c) -> (n g) c", g=K2_PASSES),
         )
+        table_probe = const.tile([P, 1], F32)
+        nc.scalar.activation(out=table_probe[:], in_=neg_half[:], func=ACT.Silu)
         load_w1(0, 1)
         load_w1(1)
         load_w2(0)
-        table_probe = const.tile([P, 1], F32)
-        nc.scalar.activation(out=table_probe[:], in_=neg_half[:], func=ACT.Silu)
-
-        def load_x_rest(first, last):
-            for b in range(first, last):
-                nc.sync.dma_start(
-                    out=x_rest[b * PAIR_ROWS : (b + 1) * PAIR_ROWS, :, :],
-                    in_=xs_mix[b, 2 * FIRST_PAIRS :].rearrange("(i e) p d -> (e p) i d", e=2),
-                )
-
+        load_xs(nc.sync, 1)
         load_w1(2)
-        load_x_rest(0, 2)
         load_w2(1)
-        load_x_rest(2, 5)
+        load_xs(nc.sync, 2)
         load_w1(3)
-        load_x_rest(5, BATCH)
         load_w2(2)
+        load_xs(nc.sync, 3)
         load_w1(4)
         load_w2(3)
+        for i in range(4, PAIRS):
+            load_xs(nc.sync, i)
 
-        def x_of(i):
-            return x_first[:, i, :] if i < FIRST_PAIRS else x_rest[:, i - FIRST_PAIRS, :]
-
-        sel_te = const.tile([P, BATCH, 2, TASKS], BF16)
+        sel_te = const.tile([P, 2, BATCH, TASKS], BF16)
         nc.vector.tensor_copy(
-            out=sel_te[:].rearrange("q b e p -> q (b e) p"),
-            in_=ident[:, TE_ROW : TE_ROW + TASKS].unsqueeze(1).to_broadcast([P, BATCH * 2, TASKS]),
+            out=sel_te[:].rearrange("q e b p -> q (e b) p"),
+            in_=ident[:, TE_ROW : TE_ROW + TASKS].unsqueeze(1).to_broadcast([P, 2 * BATCH, TASKS]),
         )
-        sel = const.tile([P, PAIRS, BATCH, 2, TASKS], BF16)
+        sel = const.tile([P, PAIRS, 2, BATCH, TASKS], BF16)
         for i in range(PAIRS):
             nc.vector.tensor_tensor(
-                out=sel[:, i],
-                in0=sel_te[:],
-                in1=ident[:, B2_ROW + 2 * i : B2_ROW + 2 * i + 2]
-                .unsqueeze(1)
-                .unsqueeze(3)
-                .to_broadcast([P, BATCH, 2, TASKS]),
+                out=sel[:, i].rearrange("q e b p -> q e (b p)"),
+                in0=sel_te[:].rearrange("q e b p -> q e (b p)"),
+                in1=ident[:, B2_ROW + 2 * i : B2_ROW + 2 * i + 2].unsqueeze(2).to_broadcast([P, 2, SLOTS]),
                 op=ALU.add,
             )
 
-        h_grouped = []
+        h_packed = []
         for e in range(2):
-            h_tile = const.tile(
-                [P, K2_PASSES, BATCH, 2, TASKS, PACK], BF16, name="h_grouped%d" % e, align_bytes=64
-            )
-            nc.vector.memset(h_tile[:], 0.0)
-            h_grouped.append(h_tile)
+            h_packed.append([])
+            for k in range(2):
+                codes = const.tile([P, K2_PASSES, P], U32, name="h_codes%d%d" % (e, k), align_bytes=64)
+                scales = const.tile([P, K2_PASSES, P], U8, name="h_scales%d%d" % (e, k), align_bytes=64)
+                nc.vector.memset(codes[:], 0)
+                nc.vector.memset(scales[:], 0)
+                h_packed[e].append((codes, scales))
 
         te_rep = const.tile([P, D], BF16)
 
         def spread_task_embedding():
             te_ps = ps_one.tile([P, D], F32, tag="spread")
             nc.tensor.matmul(
-                te_ps[:], lhsT=sel_te[:].rearrange("q b e p -> q (b e p)"), rhs=te_rows[:], start=True, stop=True
+                te_ps[:], lhsT=sel_te[:].rearrange("q e b p -> q (e b p)"), rhs=te_rows[:], start=True, stop=True
             )
             nc.vector.tensor_copy(out=te_rep[:], in_=te_ps[:])
 
@@ -245,7 +231,7 @@ def tile_hdmodel_pb_kernel(tc, xs_mix, task_emb, W1, b1, W2, b2, ln_g, ln_b, out
 
         def round_xs(i):
             xs16 = prep.tile([P, D], BF16)
-            nc.vector.tensor_tensor(out=xs16[:], in0=x_of(i), in1=te_rep[:], op=ALU.add)
+            nc.vector.tensor_tensor(out=xs16[:], in0=x_all[:, i, :], in1=te_rep[:], op=ALU.add)
             pair_tiles[("xs16", i)] = xs16
 
         def flip_xs(i):
@@ -256,40 +242,37 @@ def tile_hdmodel_pb_kernel(tc, xs_mix, task_emb, W1, b1, W2, b2, ln_g, ln_b, out
                 nc.tensor.transpose(xs_flip[:, t, :], xs16_by_t[:, t, :], ident[:])
             teb2_ps = ps_one.tile([P, D], F32, tag="spread")
             nc.tensor.matmul(
-                teb2_ps[:], lhsT=sel[:, i].rearrange("q b e p -> q (b e p)"), rhs=vec_rows[:], start=True, stop=True
+                teb2_ps[:], lhsT=sel[:, i].rearrange("q e b p -> q (e b p)"), rhs=vec_rows[:], start=True, stop=True
             )
             pair_tiles[("xs_flip", i)] = xs_flip
             pair_tiles[("teb2", i)] = teb2_ps
 
         def group_xs(i):
-            xs_grouped = prep.tile([P, 2, BATCH, TASKS, PACK], BF16, align_bytes=64)
-            xs_flip_by_e = pair_tiles[("xs_flip", i)][:].rearrange("q t (b e p) -> q e b p t", e=2, p=TASKS)
-            for e in range(2):
-                nc.scalar.copy(out=xs_grouped[:, e], in_=xs_flip_by_e[:, e])
+            xs_grouped = prep.tile([P, P, PACK], BF16, align_bytes=64)
+            nc.scalar.copy(out=xs_grouped[:], in_=pair_tiles[("xs_flip", i)][:].rearrange("q t r -> q r t"))
             pair_tiles[("xs_grouped", i)] = xs_grouped
 
         def residual_term(i):
             resid = prep.tile([P, D], F32)
-            nc.vector.tensor_tensor(out=resid[:], in0=pair_tiles[("teb2", i)][:], in1=x_of(i), op=ALU.add)
+            nc.vector.tensor_tensor(out=resid[:], in0=pair_tiles[("teb2", i)][:], in1=x_all[:, i, :], op=ALU.add)
             pair_tiles[("resid", i)] = resid
 
         def quantise_xs(i):
             xs_codes = prep.tile([P, 2 * SLOTS], U32, align_bytes=64)
             xs_scales = prep.tile([P, 2 * SLOTS], U8, align_bytes=64)
-            quantise(
-                nc, xs_codes[:], xs_scales[:], pair_tiles[("xs_grouped", i)][:].rearrange("q e b p t -> q (e b p t)")
-            )
+            quantise(nc, xs_codes[:], xs_scales[:], pair_tiles[("xs_grouped", i)][:].rearrange("q r t -> q (r t)"))
             xs_packed[i] = (xs_codes, xs_scales)
 
         def spread_gain(i):
-            gb_wide = prep.tile([P, 2 * (D // P), BATCH, PAIR_ROWS], BF16)
-            nc.scalar.copy(
-                out=gb_wide[:],
-                in_=gb_col[:]
-                .rearrange("q v c n p -> q (v c) (n p)")[:, :, i * PAIR_ROWS : (i + 1) * PAIR_ROWS]
-                .unsqueeze(2)
-                .to_broadcast([P, 2 * (D // P), BATCH, PAIR_ROWS]),
-            )
+            gb_wide = prep.tile([P, 2 * (D // P), 2, BATCH, TASKS], BF16)
+            for e in range(2):
+                nc.scalar.copy(
+                    out=gb_wide[:, :, e],
+                    in_=gb_col[:]
+                    .rearrange("q v c n p -> q (v c) n p")[:, :, 2 * i + e, :]
+                    .unsqueeze(2)
+                    .to_broadcast([P, 2 * (D // P), BATCH, TASKS]),
+                )
             pair_tiles[("gb_wide", i)] = gb_wide
 
         def flip_gain(i):
@@ -299,7 +282,7 @@ def tile_hdmodel_pb_kernel(tc, xs_mix, task_emb, W1, b1, W2, b2, ln_g, ln_b, out
                 for c in range(D // P):
                     nc.tensor.transpose(
                         gb_ps[:, v, c * P : (c + 1) * P],
-                        gb_wide[:, v * (D // P) + c].rearrange("q b s -> q (b s)"),
+                        gb_wide[:, v * (D // P) + c].rearrange("q e b p -> q (e b p)"),
                         ident[:],
                     )
             pair_tiles[("gb", i)] = gb_ps
@@ -321,9 +304,9 @@ def tile_hdmodel_pb_kernel(tc, xs_mix, task_emb, W1, b1, W2, b2, ln_g, ln_b, out
                 )
 
         def add_bias(n):
-            pre = hid.tile([P, K2_PASSES, BATCH, TASKS, PACK], F32)
+            pre = hid.tile([P, K2_PASSES, SLOTS, PACK], F32)
             nc.vector.tensor_tensor(
-                out=pre[:].rearrange("q g b p t -> q g (b p) t"),
+                out=pre[:],
                 in0=h_tiles[("h_ps", n)][:].rearrange("q (g t) r -> q g r t", t=PACK),
                 in1=b1_col[:, n].unsqueeze(2).to_broadcast([P, K2_PASSES, SLOTS, PACK]),
                 op=ALU.add,
@@ -331,25 +314,32 @@ def tile_hdmodel_pb_kernel(tc, xs_mix, task_emb, W1, b1, W2, b2, ln_g, ln_b, out
             h_tiles[("pre", n)] = pre
 
         def silu(n):
-            e = n % 2
-            nc.scalar.activation(out=h_grouped[e][:, :, :, e, :, :], in_=h_tiles[("pre", n)][:], func=ACT.Silu)
+            h_grouped = hid.tile([P, K2_PASSES, SLOTS, PACK], BF16, align_bytes=64)
+            nc.scalar.activation(out=h_grouped[:], in_=h_tiles[("pre", n)][:], func=ACT.Silu)
+            h_tiles[("grouped", n)] = h_grouped
 
         def second_matmul(n):
             i, e = divmod(n, 2)
-            h_codes = hid.tile([P, K2_PASSES * P], U32, align_bytes=64)
-            h_scales = hid.tile([P, K2_PASSES * P], U8, align_bytes=64)
-            quantise(nc, h_codes[:], h_scales[:], h_grouped[e][:].rearrange("q g b s p t -> q (g b s p t)"))
+            h_codes, h_scales = h_packed[e][i % 2]
+            mine = slice(e * SLOTS, (e + 1) * SLOTS)
+            for g in range(K2_PASSES):
+                quantise(
+                    nc,
+                    h_codes[:, g, mine],
+                    h_scales[:, g, mine],
+                    h_tiles[("grouped", n)][:, g].rearrange("q r t -> q (r t)"),
+                )
             if e == 0:
                 pair_tiles[("mlp", i)] = ps_two.tile([P, D], F32, tag="mlp", name="mlp_ps")
             for g in range(K2_PASSES):
                 codes, scales = w_packed[(2, n)]
-                mine = slice(g * D, (g + 1) * D)
+                cols = slice(g * D, (g + 1) * D)
                 nc.tensor.matmul_mx(
                     out=pair_tiles[("mlp", i)][:],
-                    lhsT=h_codes[:, g * P : (g + 1) * P].bitcast(FP8X4),
-                    lhsT_scale=h_scales[:, g * P : (g + 1) * P],
-                    rhs=codes[:, mine].bitcast(FP8X4),
-                    rhs_scale=scales[:, mine],
+                    lhsT=h_codes[:, g].bitcast(FP8X4),
+                    lhsT_scale=h_scales[:, g],
+                    rhs=codes[:, cols].bitcast(FP8X4),
+                    rhs_scale=scales[:, cols],
                     start=(e == 0 and g == 0),
                     stop=(e == 1 and g == K2_PASSES - 1),
                 )
@@ -413,11 +403,8 @@ def tile_hdmodel_pb_kernel(tc, xs_mix, task_emb, W1, b1, W2, b2, ln_g, ln_b, out
                 op0=ALU.mult,
                 op1=ALU.add,
             )
-            for b in range(BATCH):
-                nc.sync.dma_start(
-                    out=out[b, 2 * i : 2 * i + 2].rearrange("e p d -> (e p) d"),
-                    in_=y[b * PAIR_ROWS : (b + 1) * PAIR_ROWS, :],
-                )
+            for e in range(2):
+                nc.sync.dma_start(out=out[:, 2 * i + e], in_=y[e * SLOTS : (e + 1) * SLOTS, :])
 
         regroup_piece(1, 0, 0)
         spread_task_embedding()
@@ -425,7 +412,6 @@ def tile_hdmodel_pb_kernel(tc, xs_mix, task_emb, W1, b1, W2, b2, ln_g, ln_b, out
         flip_xs(0)
         regroup_piece(1, 0, 1)
         group_xs(0)
-        turn_vectors()
         for n in range(EXPERTS):
             even = n % 2 == 0
             if n + PREFETCH + 1 < EXPERTS:
@@ -449,6 +435,8 @@ def tile_hdmodel_pb_kernel(tc, xs_mix, task_emb, W1, b1, W2, b2, ln_g, ln_b, out
                 silu(n - 1)
             for piece in range(len(w_raw[(2, n)])):
                 regroup_piece(2, n, piece)
+            if n == 0:
+                turn_vectors()
 
             if not even and n >= 3:
                 add_residual(n // 2 - 1)

@@ -25,7 +25,7 @@ def vector_cols(layer, n):
     if n == 0:
         return 640
     if n == EXPERTS - 1:
-        return 256 if layer == 2 else 176
+        return 320 if layer == 2 else 176
     return 256 if layer == 1 and n >= 2 else 464
 
 GPSIMD_COLS = 224
@@ -133,9 +133,8 @@ def tile_hdmodel_pb_kernel(tc, xs_mix, task_emb, W1, b1, W2, b2, ln_g, ln_b, out
             quantise(nc, codes[:], scales[:], w_grouped[(layer, n)][:].rearrange("p w j -> p (w j)"))
             w_packed[(layer, n)] = (codes, scales)
 
-        te_rows = const.tile([P, D], BF16)
-        nc.gpsimd.memset(te_rows[:], 0.0)
-        nc.sync.dma_start(out=te_rows[TE_ROW : TE_ROW + TASKS, :], in_=task_emb)
+        te_rep = const.tile([P, D], BF16)
+        nc.sync.dma_start(out=te_rep[:], in_=task_emb.unsqueeze(0).to_broadcast([2 * BATCH, TASKS, D]))
         vec_rows = const.tile([P, D], BF16)
         nc.vector.memset(vec_rows[:], 0.0)
         ident = const.tile([P, P], BF16)
@@ -199,15 +198,6 @@ def tile_hdmodel_pb_kernel(tc, xs_mix, task_emb, W1, b1, W2, b2, ln_g, ln_b, out
                 nc.vector.memset(codes[:], 0)
                 nc.vector.memset(scales[:], 0)
                 h_packed[e].append((codes, scales))
-
-        te_rep = const.tile([P, D], BF16)
-
-        def spread_task_embedding():
-            te_ps = ps_one.tile([P, D], F32, tag="spread")
-            nc.tensor.matmul(
-                te_ps[:], lhsT=sel_te[:].rearrange("q e b p -> q (e b p)"), rhs=te_rows[:], start=True, stop=True
-            )
-            nc.vector.tensor_copy(out=te_rep[:], in_=te_ps[:])
 
         b1_col = const.tile([P, EXPERTS, K2_PASSES, PACK], F32)
         gb_col = const.tile([P, 2, D // P, EXPERTS, TASKS], BF16)
@@ -359,17 +349,19 @@ def tile_hdmodel_pb_kernel(tc, xs_mix, task_emb, W1, b1, W2, b2, ln_g, ln_b, out
             pair_tiles[("r", i)] = r
             pair_tiles[("r_sum", i)] = r_sum
 
-        def variance(i):
+        def negate_mean(i):
             neg_mean = norm.tile([P, 1], F32)
             nc.scalar.mul(neg_mean[:], pair_tiles[("r_sum", i)][:], -1.0 / D)
             pair_tiles[("neg_mean", i)] = neg_mean
+
+        def variance(i):
             squares = norm.tile([P, D], F32)
             sq_sum = norm.tile([P, 1], F32)
             nc.scalar.activation(
                 out=squares[:],
                 in_=pair_tiles[("r", i)][:],
                 func=ACT.Square,
-                bias=neg_mean[:],
+                bias=pair_tiles[("neg_mean", i)][:],
                 scale=1.0,
                 accum_out=sq_sum[:],
             )
@@ -407,7 +399,6 @@ def tile_hdmodel_pb_kernel(tc, xs_mix, task_emb, W1, b1, W2, b2, ln_g, ln_b, out
                 nc.sync.dma_start(out=out[:, 2 * i + e], in_=y[e * SLOTS : (e + 1) * SLOTS, :])
 
         regroup_piece(1, 0, 0)
-        spread_task_embedding()
         round_xs(0)
         flip_xs(0)
         regroup_piece(1, 0, 1)
@@ -455,21 +446,25 @@ def tile_hdmodel_pb_kernel(tc, xs_mix, task_emb, W1, b1, W2, b2, ln_g, ln_b, out
                 second_matmul(n - 1)
             if even and n + 2 < EXPERTS:
                 round_xs(n // 2 + 1)
+            if not even and n >= 3:
+                negate_mean(n // 2 - 1)
             if not even and n + 1 < EXPERTS:
                 group_xs(n // 2 + 1)
+            if n == EXPERTS - 1:
+                silu(n)
             if not even and n >= 3:
                 variance(n // 2 - 1)
             if even and n >= 2:
                 spread_gain(n // 2 - 1)
 
         last = EXPERTS - 1
-        silu(last)
         spread_gain(PAIRS - 1)
         quantise_weight(2, last)
         second_matmul(last)
         flip_gain(PAIRS - 1)
         centre_times_gain(PAIRS - 2)
         add_residual(PAIRS - 1)
+        negate_mean(PAIRS - 1)
         variance(PAIRS - 1)
         normalise_and_store(PAIRS - 2)
         centre_times_gain(PAIRS - 1)

@@ -25,8 +25,8 @@ def vector_cols(layer, n):
     if n == 0:
         return 640
     if n == EXPERTS - 1:
-        return 320 if layer == 2 else 176
-    return 256 if layer == 1 and n >= 2 else 464
+        return 288 if layer == 2 else 144
+    return 224 if layer == 1 and n >= 2 else 432
 
 GPSIMD_COLS = 224
 RUN = 2
@@ -133,8 +133,9 @@ def tile_hdmodel_pb_kernel(tc, xs_mix, task_emb, W1, b1, W2, b2, ln_g, ln_b, out
             quantise(nc, codes[:], scales[:], w_grouped[(layer, n)][:].rearrange("p w j -> p (w j)"))
             w_packed[(layer, n)] = (codes, scales)
 
-        te_rep = const.tile([P, D], BF16)
-        nc.sync.dma_start(out=te_rep[:], in_=task_emb.unsqueeze(0).to_broadcast([2 * BATCH, TASKS, D]))
+        te_rows = const.tile([P, D], BF16)
+        nc.gpsimd.memset(te_rows[:], 0.0)
+        nc.sync.dma_start(out=te_rows[TE_ROW : TE_ROW + TASKS, :], in_=task_emb)
         vec_rows = const.tile([P, D], BF16)
         nc.vector.memset(vec_rows[:], 0.0)
         ident = const.tile([P, P], BF16)
@@ -198,6 +199,15 @@ def tile_hdmodel_pb_kernel(tc, xs_mix, task_emb, W1, b1, W2, b2, ln_g, ln_b, out
                 nc.vector.memset(codes[:], 0)
                 nc.vector.memset(scales[:], 0)
                 h_packed[e].append((codes, scales))
+
+        te_rep = const.tile([P, D], BF16)
+
+        def spread_task_embedding():
+            te_ps = ps_one.tile([P, D], F32, tag="spread")
+            nc.tensor.matmul(
+                te_ps[:], lhsT=sel_te[:].rearrange("q e b p -> q (e b p)"), rhs=te_rows[:], start=True, stop=True
+            )
+            nc.vector.tensor_copy(out=te_rep[:], in_=te_ps[:])
 
         b1_col = const.tile([P, EXPERTS, K2_PASSES, PACK], F32)
         gb_col = const.tile([P, 2, D // P, EXPERTS, TASKS], BF16)
@@ -399,6 +409,7 @@ def tile_hdmodel_pb_kernel(tc, xs_mix, task_emb, W1, b1, W2, b2, ln_g, ln_b, out
                 nc.sync.dma_start(out=out[:, 2 * i + e], in_=y[e * SLOTS : (e + 1) * SLOTS, :])
 
         regroup_piece(1, 0, 0)
+        spread_task_embedding()
         round_xs(0)
         flip_xs(0)
         regroup_piece(1, 0, 1)

@@ -25,10 +25,11 @@ def vector_cols(layer, n):
     if n == 0:
         return 640
     if n == EXPERTS - 1:
-        return 288 if layer == 2 else 144
-    return 224 if layer == 1 and n >= 2 else 432
+        return 256 if layer == 2 else 96
+    return VECTOR_AND_GPSIMD - gpsimd_cols(1, n) if layer == 1 and n >= 2 else 432
 
-GPSIMD_COLS = 224
+VECTOR_AND_GPSIMD = 432
+GPSIMD_EVEN, GPSIMD_ODD = 176, 336
 RUN = 2
 
 TE_ROW, B2_ROW, G_ROW, B_ROW, B1_ROW = 0, 8, 32, 48, 64
@@ -39,7 +40,9 @@ FLOPS = 2 * EXPERTS * SLOTS * D * H * 2
 
 
 def gpsimd_cols(layer, n):
-    return GPSIMD_COLS if layer == 1 and n >= 2 else 0
+    if layer == 2 or n < 2:
+        return 0
+    return GPSIMD_ODD if n % 2 else GPSIMD_EVEN
 
 
 def regroup(nc, grouped, rows, vector_end, scalar_first):
@@ -200,15 +203,6 @@ def tile_hdmodel_pb_kernel(tc, xs_mix, task_emb, W1, b1, W2, b2, ln_g, ln_b, out
                 nc.vector.memset(scales[:], 0)
                 h_packed[e].append((codes, scales))
 
-        te_rep = const.tile([P, D], BF16)
-
-        def spread_task_embedding():
-            te_ps = ps_one.tile([P, D], F32, tag="spread")
-            nc.tensor.matmul(
-                te_ps[:], lhsT=sel_te[:].rearrange("q e b p -> q (e b p)"), rhs=te_rows[:], start=True, stop=True
-            )
-            nc.vector.tensor_copy(out=te_rep[:], in_=te_ps[:])
-
         b1_col = const.tile([P, EXPERTS, K2_PASSES, PACK], F32)
         gb_col = const.tile([P, 2, D // P, EXPERTS, TASKS], BF16)
 
@@ -229,27 +223,39 @@ def tile_hdmodel_pb_kernel(tc, xs_mix, task_emb, W1, b1, W2, b2, ln_g, ln_b, out
                     .to_broadcast([P, D // P, EXPERTS, TASKS]),
                 )
 
-        def round_xs(i):
-            xs16 = prep.tile([P, D], BF16)
-            nc.vector.tensor_tensor(out=xs16[:], in0=x_all[:, i, :], in1=te_rep[:], op=ALU.add)
-            pair_tiles[("xs16", i)] = xs16
+        te_col = const.tile([P, TASKS, PACK], BF16)
+
+        def turn_task_embedding():
+            te_ps = ps_two.tile([P, PACK, P], BF16, tag="gb")
+            rows_by_t = te_rows[:].rearrange("r (q t) -> r t q", t=PACK)
+            for t in range(PACK):
+                nc.tensor.transpose(te_ps[:, t, :], rows_by_t[:, t, :], ident[:])
+            nc.vector.tensor_copy(
+                out=te_col[:], in_=te_ps[:, :, TE_ROW : TE_ROW + TASKS].rearrange("q t p -> q p t")
+            )
 
         def flip_xs(i):
-            xs16 = pair_tiles[("xs16", i)]
             xs_flip = ps_one.tile([P, PACK, P], BF16, tag="flip")
-            xs16_by_t = xs16[:].rearrange("r (q t) -> r t q", t=PACK)
+            x_by_t = x_all[:, i, :].rearrange("r (q t) -> r t q", t=PACK)
             for t in range(PACK):
-                nc.tensor.transpose(xs_flip[:, t, :], xs16_by_t[:, t, :], ident[:])
+                nc.tensor.transpose(xs_flip[:, t, :], x_by_t[:, t, :], ident[:])
+            pair_tiles[("xs_flip", i)] = xs_flip
+
+        def spread_bias(i):
             teb2_ps = ps_one.tile([P, D], F32, tag="spread")
             nc.tensor.matmul(
                 teb2_ps[:], lhsT=sel[:, i].rearrange("q e b p -> q (e b p)"), rhs=vec_rows[:], start=True, stop=True
             )
-            pair_tiles[("xs_flip", i)] = xs_flip
             pair_tiles[("teb2", i)] = teb2_ps
 
-        def group_xs(i):
-            xs_grouped = prep.tile([P, P, PACK], BF16, align_bytes=64)
-            nc.scalar.copy(out=xs_grouped[:], in_=pair_tiles[("xs_flip", i)][:].rearrange("q t r -> q r t"))
+        def add_task_embedding(i):
+            xs_grouped = prep.tile([P, 2 * BATCH, TASKS, PACK], BF16, align_bytes=64)
+            nc.vector.tensor_tensor(
+                out=xs_grouped[:],
+                in0=pair_tiles[("xs_flip", i)][:].rearrange("q t (s p) -> q s p t", p=TASKS),
+                in1=te_col[:].unsqueeze(1).to_broadcast([P, 2 * BATCH, TASKS, PACK]),
+                op=ALU.add,
+            )
             pair_tiles[("xs_grouped", i)] = xs_grouped
 
         def residual_term(i):
@@ -260,20 +266,19 @@ def tile_hdmodel_pb_kernel(tc, xs_mix, task_emb, W1, b1, W2, b2, ln_g, ln_b, out
         def quantise_xs(i):
             xs_codes = prep.tile([P, 2 * SLOTS], U32, align_bytes=64)
             xs_scales = prep.tile([P, 2 * SLOTS], U8, align_bytes=64)
-            quantise(nc, xs_codes[:], xs_scales[:], pair_tiles[("xs_grouped", i)][:].rearrange("q r t -> q (r t)"))
+            quantise(nc, xs_codes[:], xs_scales[:], pair_tiles[("xs_grouped", i)][:].rearrange("q s p t -> q (s p t)"))
             xs_packed[i] = (xs_codes, xs_scales)
 
-        def spread_gain(i):
-            gb_wide = prep.tile([P, 2 * (D // P), 2, BATCH, TASKS], BF16)
-            for e in range(2):
-                nc.scalar.copy(
-                    out=gb_wide[:, :, e],
-                    in_=gb_col[:]
-                    .rearrange("q v c n p -> q (v c) n p")[:, :, 2 * i + e, :]
-                    .unsqueeze(2)
-                    .to_broadcast([P, 2 * (D // P), BATCH, TASKS]),
-                )
-            pair_tiles[("gb_wide", i)] = gb_wide
+        def spread_gain(i, e):
+            if e == 0:
+                pair_tiles[("gb_wide", i)] = prep.tile([P, 2 * (D // P), 2, BATCH, TASKS], BF16, name="gb_wide")
+            nc.scalar.copy(
+                out=pair_tiles[("gb_wide", i)][:, :, e],
+                in_=gb_col[:]
+                .rearrange("q v c n p -> q (v c) n p")[:, :, 2 * i + e, :]
+                .unsqueeze(2)
+                .to_broadcast([P, 2 * (D // P), BATCH, TASKS]),
+            )
 
         def flip_gain(i):
             gb_wide = pair_tiles[("gb_wide", i)]
@@ -375,12 +380,18 @@ def tile_hdmodel_pb_kernel(tc, xs_mix, task_emb, W1, b1, W2, b2, ln_g, ln_b, out
                 scale=1.0,
                 accum_out=sq_sum[:],
             )
+            pair_tiles[("sq_sum", i)] = sq_sum
+
+        def inverse_deviation(i):
             var_eps = norm.tile([P, 1], F32)
-            nc.gpsimd.tensor_scalar(
-                out=var_eps[:], in0=sq_sum[:], scalar1=1.0 / D, scalar2=EPS, op0=ALU.mult, op1=ALU.add
+            nc.scalar.activation(
+                out=var_eps[:], in_=pair_tiles[("sq_sum", i)][:], func=ACT.Identity, scale=1.0 / D, bias=EPS
             )
+            pair_tiles[("var_eps", i)] = var_eps
+
+        def inverse_root(i):
             rstd = norm.tile([P, 1], F32)
-            nc.gpsimd.tensor_tensor(out=rstd[:], in0=var_eps[:], in1=neg_half[:], op=ALU.pow)
+            nc.gpsimd.tensor_tensor(out=rstd[:], in0=pair_tiles[("var_eps", i)][:], in1=neg_half[:], op=ALU.pow)
             pair_tiles[("rstd", i)] = rstd
 
         def centre_times_gain(i):
@@ -409,11 +420,11 @@ def tile_hdmodel_pb_kernel(tc, xs_mix, task_emb, W1, b1, W2, b2, ln_g, ln_b, out
                 nc.sync.dma_start(out=out[:, 2 * i + e], in_=y[e * SLOTS : (e + 1) * SLOTS, :])
 
         regroup_piece(1, 0, 0)
-        spread_task_embedding()
-        round_xs(0)
+        turn_task_embedding()
         flip_xs(0)
+        spread_bias(0)
         regroup_piece(1, 0, 1)
-        group_xs(0)
+        add_task_embedding(0)
         for n in range(EXPERTS):
             even = n % 2 == 0
             if n + PREFETCH + 1 < EXPERTS:
@@ -429,8 +440,12 @@ def tile_hdmodel_pb_kernel(tc, xs_mix, task_emb, W1, b1, W2, b2, ln_g, ln_b, out
             first_matmul(n)
             if n + 2 < EXPERTS:
                 gpsimd_share(1, n + 2)
-            if not even and n + 1 < EXPERTS:
+            if even and n >= 4:
+                inverse_root(n // 2 - 2)
+            if even and n + 2 < EXPERTS:
                 flip_xs(n // 2 + 1)
+            if not even and n + 1 < EXPERTS:
+                spread_bias(n // 2 + 1)
             if not even and n >= 3:
                 flip_gain(n // 2 - 1)
             if n >= 1:
@@ -440,6 +455,8 @@ def tile_hdmodel_pb_kernel(tc, xs_mix, task_emb, W1, b1, W2, b2, ln_g, ln_b, out
             if n == 0:
                 turn_vectors()
 
+            if not even and n >= 5:
+                normalise_and_store(n // 2 - 2)
             if not even and n >= 3:
                 add_residual(n // 2 - 1)
             if even and n >= 4:
@@ -449,27 +466,26 @@ def tile_hdmodel_pb_kernel(tc, xs_mix, task_emb, W1, b1, W2, b2, ln_g, ln_b, out
             if not even and n + 1 < EXPERTS:
                 residual_term(n // 2 + 1)
             add_bias(n)
-            if even and n >= 4:
-                normalise_and_store(n // 2 - 2)
+            if even and n + 2 < EXPERTS:
+                add_task_embedding(n // 2 + 1)
 
             if n >= 1:
                 quantise_weight(2, n - 1)
                 second_matmul(n - 1)
-            if even and n + 2 < EXPERTS:
-                round_xs(n // 2 + 1)
             if not even and n >= 3:
                 negate_mean(n // 2 - 1)
-            if not even and n + 1 < EXPERTS:
-                group_xs(n // 2 + 1)
+            if not even:
+                spread_gain(n // 2, 0)
             if n == EXPERTS - 1:
                 silu(n)
             if not even and n >= 3:
                 variance(n // 2 - 1)
-            if even and n >= 2:
-                spread_gain(n // 2 - 1)
+            if not even:
+                spread_gain(n // 2, 1)
+            if not even and n >= 3:
+                inverse_deviation(n // 2 - 1)
 
         last = EXPERTS - 1
-        spread_gain(PAIRS - 1)
         quantise_weight(2, last)
         second_matmul(last)
         flip_gain(PAIRS - 1)
@@ -477,6 +493,9 @@ def tile_hdmodel_pb_kernel(tc, xs_mix, task_emb, W1, b1, W2, b2, ln_g, ln_b, out
         add_residual(PAIRS - 1)
         negate_mean(PAIRS - 1)
         variance(PAIRS - 1)
+        inverse_root(PAIRS - 2)
+        inverse_deviation(PAIRS - 1)
+        inverse_root(PAIRS - 1)
         normalise_and_store(PAIRS - 2)
         centre_times_gain(PAIRS - 1)
         normalise_and_store(PAIRS - 1)

@@ -25,11 +25,14 @@ def vector_cols(layer, n):
     if n == 0:
         return 640
     if n == EXPERTS - 1:
-        return 256 if layer == 2 else 96
+        return 160 if layer == 2 else 96
+    if layer == 2 and n == EXPERTS - 2:
+        return 304
     return VECTOR_AND_GPSIMD - gpsimd_cols(1, n) if layer == 1 and n >= 2 else 432
 
 VECTOR_AND_GPSIMD = 432
 GPSIMD_EVEN, GPSIMD_ODD = 176, 336
+GPSIMD_W2 = 128
 RUN = 2
 
 TE_ROW, B2_ROW, G_ROW, B_ROW, B1_ROW = 0, 8, 32, 48, 64
@@ -40,7 +43,9 @@ FLOPS = 2 * EXPERTS * SLOTS * D * H * 2
 
 
 def gpsimd_cols(layer, n):
-    if layer == 2 or n < 2:
+    if layer == 2:
+        return GPSIMD_W2 if n >= EXPERTS - 2 else 0
+    if n < 2:
         return 0
     return GPSIMD_ODD if n % 2 else GPSIMD_EVEN
 
@@ -129,6 +134,9 @@ def tile_hdmodel_pb_kernel(tc, xs_mix, task_emb, W1, b1, W2, b2, ln_g, ln_b, out
                 vector_end,
                 vector_end + gpsimd_cols(layer, n),
             )
+            if layer == 2 and gpsimd_cols(layer, n):
+                mine = slice(vector_end - RUN, vector_end + gpsimd_cols(layer, n))
+                regroup_on_gpsimd(nc, w_grouped[(layer, n)][:, mine, :], view[:, :, mine])
 
         def quantise_weight(layer, n):
             codes = wq.tile([P, COLS], U32, tag="codes%d" % layer, align_bytes=64)
@@ -138,7 +146,6 @@ def tile_hdmodel_pb_kernel(tc, xs_mix, task_emb, W1, b1, W2, b2, ln_g, ln_b, out
 
         te_rows = const.tile([P, D], BF16)
         nc.gpsimd.memset(te_rows[:], 0.0)
-        nc.sync.dma_start(out=te_rows[TE_ROW : TE_ROW + TASKS, :], in_=task_emb)
         vec_rows = const.tile([P, D], BF16)
         nc.vector.memset(vec_rows[:], 0.0)
         ident = const.tile([P, P], BF16)
@@ -153,6 +160,7 @@ def tile_hdmodel_pb_kernel(tc, xs_mix, task_emb, W1, b1, W2, b2, ln_g, ln_b, out
                 queue.dma_start(out=x_all[e * SLOTS : (e + 1) * SLOTS, i, :], in_=xs_mix[:, 2 * i + e])
 
         load_w1(0, 0)
+        nc.sync.dma_start(out=te_rows[TE_ROW : TE_ROW + TASKS, :], in_=task_emb)
         load_xs(nc.scalar, 0)
         nc.scalar.dma_start(out=vec_rows[TE_ROW : TE_ROW + TASKS, :], in_=task_emb)
         nc.scalar.dma_start(out=vec_rows[B2_ROW : B2_ROW + EXPERTS, :], in_=b2)
@@ -389,6 +397,13 @@ def tile_hdmodel_pb_kernel(tc, xs_mix, task_emb, W1, b1, W2, b2, ln_g, ln_b, out
             )
             pair_tiles[("var_eps", i)] = var_eps
 
+        def inverse_root_on_scalar(i):
+            rstd = norm.tile([P, 1], F32)
+            nc.scalar.activation(
+                out=rstd[:], in_=pair_tiles[("sq_sum", i)][:], func=ACT.Abs_reciprocal_sqrt, scale=1.0 / D, bias=EPS
+            )
+            pair_tiles[("rstd", i)] = rstd
+
         def inverse_root(i):
             rstd = norm.tile([P, 1], F32)
             nc.gpsimd.tensor_tensor(out=rstd[:], in0=pair_tiles[("var_eps", i)][:], in1=neg_half[:], op=ALU.pow)
@@ -482,10 +497,11 @@ def tile_hdmodel_pb_kernel(tc, xs_mix, task_emb, W1, b1, W2, b2, ln_g, ln_b, out
                 variance(n // 2 - 1)
             if not even:
                 spread_gain(n // 2, 1)
-            if not even and n >= 3:
+            if not even and n >= 3 and n < EXPERTS - 1:
                 inverse_deviation(n // 2 - 1)
 
         last = EXPERTS - 1
+        inverse_root_on_scalar(PAIRS - 2)
         quantise_weight(2, last)
         second_matmul(last)
         flip_gain(PAIRS - 1)
@@ -493,9 +509,7 @@ def tile_hdmodel_pb_kernel(tc, xs_mix, task_emb, W1, b1, W2, b2, ln_g, ln_b, out
         add_residual(PAIRS - 1)
         negate_mean(PAIRS - 1)
         variance(PAIRS - 1)
-        inverse_root(PAIRS - 2)
-        inverse_deviation(PAIRS - 1)
-        inverse_root(PAIRS - 1)
+        inverse_root_on_scalar(PAIRS - 1)
         normalise_and_store(PAIRS - 2)
         centre_times_gain(PAIRS - 1)
         normalise_and_store(PAIRS - 1)

@@ -21,18 +21,8 @@ K2_PASSES = H // (P * PACK)
 EPS = 1e-5
 
 COLS = 1024
-def vector_cols(layer, n):
-    if n == 0:
-        return 640
-    if n == EXPERTS - 1:
-        return 160 if layer == 2 else 96
-    if layer == 2 and n == EXPERTS - 2:
-        return 304
-    return VECTOR_AND_GPSIMD - gpsimd_cols(1, n) if layer == 1 and n >= 2 else 432
-
 VECTOR_AND_GPSIMD = 432
-GPSIMD_EVEN, GPSIMD_ODD = 176, 336
-GPSIMD_W2 = 128
+
 RUN = 2
 
 TE_ROW, B2_ROW, G_ROW, B_ROW, B1_ROW = 0, 8, 32, 48, 64
@@ -42,12 +32,29 @@ PREFETCH = 4
 FLOPS = 2 * EXPERTS * SLOTS * D * H * 2
 
 
+def psum_reads(n):
+    if n % 2:
+        return 1 + (n >= 5) + (n >= 3) + (n + 1 < EXPERTS)
+    return 1 + (n >= 4) + (n + 2 < EXPERTS) + (n == 0)
+
+
 def gpsimd_cols(layer, n):
-    if layer == 2:
-        return GPSIMD_W2 if n >= EXPERTS - 2 else 0
-    if n < 2:
+    if layer == 1:
+        round_of = n - 2
+    else:
+        round_of = n if n >= EXPERTS - 2 else -1
+    if round_of < 0:
         return 0
-    return GPSIMD_ODD if n % 2 else GPSIMD_EVEN
+    has_root = round_of % 2 == 0 and round_of >= 4
+    return 96 * psum_reads(round_of) - (112 if has_root else 48)
+
+
+def vector_cols(layer, n):
+    if n == 0:
+        return 640
+    if n == EXPERTS - 1:
+        return 96 if layer == 2 else 96
+    return VECTOR_AND_GPSIMD - gpsimd_cols(layer, n)
 
 
 def regroup(nc, grouped, rows, vector_end, scalar_first):
@@ -184,6 +191,7 @@ def tile_hdmodel_pb_kernel(tc, xs_mix, task_emb, W1, b1, W2, b2, ln_g, ln_b, out
         load_xs(nc.sync, 3)
         load_w1(4)
         load_w2(3)
+        load_w1(5)
         for i in range(4, PAIRS):
             load_xs(nc.sync, i)
 
@@ -442,10 +450,10 @@ def tile_hdmodel_pb_kernel(tc, xs_mix, task_emb, W1, b1, W2, b2, ln_g, ln_b, out
         add_task_embedding(0)
         for n in range(EXPERTS):
             even = n % 2 == 0
-            if n + PREFETCH + 1 < EXPERTS:
-                load_w1(n + PREFETCH + 1)
             if n + PREFETCH < EXPERTS:
                 load_w2(n + PREFETCH)
+            if n + PREFETCH + 2 < EXPERTS:
+                load_w1(n + PREFETCH + 2)
 
             if n + 1 < EXPERTS:
                 regroup_piece(1, n + 1, 0)
@@ -455,7 +463,7 @@ def tile_hdmodel_pb_kernel(tc, xs_mix, task_emb, W1, b1, W2, b2, ln_g, ln_b, out
             first_matmul(n)
             if n + 2 < EXPERTS:
                 gpsimd_share(1, n + 2)
-            if even and n >= 4:
+            if even and 4 <= n < EXPERTS - 2:
                 inverse_root(n // 2 - 2)
             if even and n + 2 < EXPERTS:
                 flip_xs(n // 2 + 1)
@@ -467,6 +475,8 @@ def tile_hdmodel_pb_kernel(tc, xs_mix, task_emb, W1, b1, W2, b2, ln_g, ln_b, out
                 silu(n - 1)
             for piece in range(len(w_raw[(2, n)])):
                 regroup_piece(2, n, piece)
+            if n == EXPERTS - 2:
+                inverse_root(n // 2 - 2)
             if n == 0:
                 turn_vectors()
 

from contextlib import ExitStack

import concourse.mybir as mybir
from concourse.masks import make_identity

F32 = mybir.dt.float32
BF16 = mybir.dt.bfloat16
U32 = mybir.dt.uint32
U8 = mybir.dt.uint8
FP8X4 = mybir.dt.float8_e4m3fn_x4
ALU = mybir.AluOpType
ACT = mybir.ActivationFunctionType

P = 128
PACK = 4
BATCH, EXPERTS, TASKS, D, H = 8, 16, 8, 512, 1024
SLOTS = BATCH * TASKS
PAIRS = EXPERTS // 2
H_TILES = H // P
K2_PASSES = H // (P * PACK)
EPS = 1e-5

COLS = 1024
VECTOR_AND_GPSIMD = 432

RUN = 2

TE_ROW, B2_ROW, G_ROW, B_ROW, B1_ROW = 0, 8, 32, 48, 64

PREFETCH = 4

FLOPS = 2 * EXPERTS * SLOTS * D * H * 2


def psum_reads(n):
    if n % 2:
        return 1 + (n >= 5) + (n >= 3) + (n + 1 < EXPERTS)
    return 1 + (n >= 4) + (n + 2 < EXPERTS) + (n == 0)


def gpsimd_cols(layer, n):
    if layer == 1:
        round_of = n - 2
    else:
        round_of = n if n >= EXPERTS - 2 else -1
    if round_of < 0:
        return 0
    has_root = round_of % 2 == 0 and round_of >= 4
    return 96 * psum_reads(round_of) - (112 if has_root else 48)


def vector_cols(layer, n):
    if n == 0:
        return 640
    if n == EXPERTS - 1:
        return 96 if layer == 2 else 96
    return VECTOR_AND_GPSIMD - gpsimd_cols(layer, n)


def regroup(nc, grouped, rows, vector_end, scalar_first):
    dst = grouped.rearrange("p (c i) j -> p c j i", i=RUN)
    src = rows.rearrange("p j (c i) -> p c j i", i=RUN)
    a, b = vector_end // RUN, scalar_first // RUN
    nc.vector.tensor_copy(out=dst[:, :a], in_=src[:, :a])
    nc.scalar.copy(out=dst[:, b:], in_=src[:, b:])


def regroup_on_gpsimd(nc, grouped, rows):
    nc.gpsimd.tensor_scalar(
        out=grouped, in0=rows.rearrange("p j w -> p w j"), scalar1=1.0, scalar2=0.0, op0=ALU.mult, op1=ALU.add
    )


def quantise(nc, codes, scales, grouped):
    nc.vector.quantize_mx(out=codes.bitcast(FP8X4), scales=scales, in_=grouped)


def tile_hdmodel_pb_kernel(tc, xs_mix, task_emb, W1, b1, W2, b2, ln_g, ln_b, out):
    nc = tc.nc
    with ExitStack() as ctx:
        const = ctx.enter_context(tc.tile_pool(name="const", bufs=1))
        raw = ctx.enter_context(tc.tile_pool(name="raw", bufs=PREFETCH + 1))
        stage = ctx.enter_context(tc.tile_pool(name="stage", bufs=2))
        wq = ctx.enter_context(tc.tile_pool(name="wq", bufs=3))
        prep = ctx.enter_context(tc.tile_pool(name="prep", bufs=3))
        hid = ctx.enter_context(tc.tile_pool(name="hid", bufs=2))
        norm = ctx.enter_context(tc.tile_pool(name="norm", bufs=2))
        ps_one = ctx.enter_context(tc.psum_pool(name="ps_one", bufs=1))
        ps_two = ctx.enter_context(tc.psum_pool(name="ps_two", bufs=2))
        ctx.enter_context(tc.manual_schedule())

        w_raw = {}
        w_grouped = {}
        w_packed = {}
        xs_packed = {}
        pair_tiles = {}
        h_tiles = {}

        def load_w1(n, half=None):
            first, width = (0, COLS) if half is None else (half * COLS // 2, COLS // 2)
            if half is None:
                w1_raw = raw.tile([P, PACK, width], BF16, tag="raw1")
            else:
                w1_raw = const.tile([P, PACK, width], BF16, name="raw1_half%d" % half)
            nc.sync.dma_start(
                out=w1_raw[:], in_=W1[n].rearrange("(p j) h -> p j h", j=PACK)[:, :, first : first + width]
            )
            w_raw.setdefault((1, n), []).append((first, width, w1_raw[:]))

        def load_w2(n):
            w2_raw = raw.tile([P, PACK, K2_PASSES, D], BF16, tag="raw2")
            w2_rows = W2[n].rearrange("(g t p) d -> g p t d", g=K2_PASSES, p=P)
            for g in range(K2_PASSES):
                nc.sync.dma_start(out=w2_raw[:, :, g, :], in_=w2_rows[g])
            if n == 0:
                w_raw[(2, n)] = [(g * D, D, w2_raw[:, :, g, :]) for g in range(K2_PASSES)]
            else:
                w_raw[(2, n)] = [(0, COLS, w2_raw[:].rearrange("p t g d -> p t (g d)"))]

        def new_grouped(layer, n):
            w_grouped[(layer, n)] = stage.tile(
                [P, COLS, PACK], BF16, tag="grouped%d" % layer, name="grouped", align_bytes=64
            )

        def gpsimd_share(layer, n):
            new_grouped(layer, n)
            first = vector_cols(layer, n)
            mine = slice(first, first + gpsimd_cols(layer, n))
            ((start, width, view),) = w_raw[(layer, n)]
            regroup_on_gpsimd(nc, w_grouped[(layer, n)][:, mine, :], view[:, :, mine])

        def regroup_piece(layer, n, piece):
            if (layer, n) not in w_grouped:
                new_grouped(layer, n)
            first, width, view = w_raw[(layer, n)][piece]
            vector_end = vector_cols(layer, n) * width // COLS
            regroup(
                nc,
                w_grouped[(layer, n)][:, first : first + width],
                view,
                vector_end,
                vector_end + gpsimd_cols(layer, n),
            )
            if layer == 2 and gpsimd_cols(layer, n):
                mine = slice(vector_end - RUN, vector_end + gpsimd_cols(layer, n))
                regroup_on_gpsimd(nc, w_grouped[(layer, n)][:, mine, :], view[:, :, mine])

        def quantise_weight(layer, n):
            codes = wq.tile([P, COLS], U32, tag="codes%d" % layer, align_bytes=64)
            scales = wq.tile([P, COLS], U8, tag="scales%d" % layer, align_bytes=64)
            quantise(nc, codes[:], scales[:], w_grouped[(layer, n)][:].rearrange("p w j -> p (w j)"))
            w_packed[(layer, n)] = (codes, scales)

        te_rows = const.tile([P, D], BF16)
        nc.gpsimd.memset(te_rows[:], 0.0)
        vec_rows = const.tile([P, D], BF16)
        nc.vector.memset(vec_rows[:], 0.0)
        ident = const.tile([P, P], BF16)
        make_identity(nc, ident[:])
        neg_half = const.tile([P, 1], F32)
        nc.gpsimd.memset(neg_half[:], -0.5)

        x_all = const.tile([P, PAIRS, D], BF16)

        def load_xs(queue, i):
            for e in range(2):
                queue.dma_start(out=x_all[e * SLOTS : (e + 1) * SLOTS, i, :], in_=xs_mix[:, 2 * i + e])

        load_w1(0, 0)
        nc.sync.dma_start(out=te_rows[TE_ROW : TE_ROW + TASKS, :], in_=task_emb)
        load_xs(nc.scalar, 0)
        nc.scalar.dma_start(out=vec_rows[TE_ROW : TE_ROW + TASKS, :], in_=task_emb)
        nc.scalar.dma_start(out=vec_rows[B2_ROW : B2_ROW + EXPERTS, :], in_=b2)
        nc.scalar.dma_start(out=vec_rows[G_ROW : G_ROW + EXPERTS, :], in_=ln_g)
        nc.scalar.dma_start(out=vec_rows[B_ROW : B_ROW + EXPERTS, :], in_=ln_b)
        nc.scalar.dma_start(
            out=vec_rows[B1_ROW : B1_ROW + 2 * EXPERTS, :],
            in_=b1.rearrange("n (g c) -> (n g) c", g=K2_PASSES),
        )
        table_probe = const.tile([P, 1], F32)
        nc.scalar.activation(out=table_probe[:], in_=neg_half[:], func=ACT.Silu)
        load_w1(0, 1)
        load_w1(1)
        load_w2(0)
        load_xs(nc.sync, 1)
        load_w1(2)
        load_w2(1)
        load_xs(nc.sync, 2)
        load_w1(3)
        load_w2(2)
        load_xs(nc.sync, 3)
        load_w1(4)
        load_w2(3)
        load_w1(5)
        for i in range(4, PAIRS):
            load_xs(nc.sync, i)

        sel_te = const.tile([P, 2, BATCH, TASKS], BF16)
        nc.vector.tensor_copy(
            out=sel_te[:].rearrange("q e b p -> q (e b) p"),
            in_=ident[:, TE_ROW : TE_ROW + TASKS].unsqueeze(1).to_broadcast([P, 2 * BATCH, TASKS]),
        )
        sel = const.tile([P, PAIRS, 2, BATCH, TASKS], BF16)
        for i in range(PAIRS):
            nc.vector.tensor_tensor(
                out=sel[:, i].rearrange("q e b p -> q e (b p)"),
                in0=sel_te[:].rearrange("q e b p -> q e (b p)"),
                in1=ident[:, B2_ROW + 2 * i : B2_ROW + 2 * i + 2].unsqueeze(2).to_broadcast([P, 2, SLOTS]),
                op=ALU.add,
            )

        h_packed = []
        for e in range(2):
            h_packed.append([])
            for k in range(2):
                codes = const.tile([P, K2_PASSES, P], U32, name="h_codes%d%d" % (e, k), align_bytes=64)
                scales = const.tile([P, K2_PASSES, P], U8, name="h_scales%d%d" % (e, k), align_bytes=64)
                nc.vector.memset(codes[:], 0)
                nc.vector.memset(scales[:], 0)
                h_packed[e].append((codes, scales))

        b1_col = const.tile([P, EXPERTS, K2_PASSES, PACK], F32)
        gb_col = const.tile([P, 2, D // P, EXPERTS, TASKS], BF16)

        def turn_vectors():
            vec_cols_ps = ps_two.tile([P, PACK, P], BF16, tag="gb")
            for c in range(D // P):
                nc.tensor.transpose(vec_cols_ps[:, c, :], vec_rows[:, c * P : (c + 1) * P], ident[:])
            nc.vector.tensor_copy(
                out=b1_col[:],
                in_=vec_cols_ps[:, :, B1_ROW : B1_ROW + 2 * EXPERTS].rearrange("q t (n g) -> q n g t", g=K2_PASSES),
            )
            for v in range(2):
                first = G_ROW + v * EXPERTS
                nc.vector.tensor_copy(
                    out=gb_col[:, v],
                    in_=vec_cols_ps[:, :, first : first + EXPERTS]
                    .unsqueeze(3)
                    .to_broadcast([P, D // P, EXPERTS, TASKS]),
                )

        te_col = const.tile([P, TASKS, PACK], BF16)

        def turn_task_embedding():
            te_ps = ps_two.tile([P, PACK, P], BF16, tag="gb")
            rows_by_t = te_rows[:].rearrange("r (q t) -> r t q", t=PACK)
            for t in range(PACK):
                nc.tensor.transpose(te_ps[:, t, :], rows_by_t[:, t, :], ident[:])
            nc.vector.tensor_copy(
                out=te_col[:], in_=te_ps[:, :, TE_ROW : TE_ROW + TASKS].rearrange("q t p -> q p t")
            )

        def flip_xs(i):
            xs_flip = ps_one.tile([P, PACK, P], BF16, tag="flip")
            x_by_t = x_all[:, i, :].rearrange("r (q t) -> r t q", t=PACK)
            for t in range(PACK):
                nc.tensor.transpose(xs_flip[:, t, :], x_by_t[:, t, :], ident[:])
            pair_tiles[("xs_flip", i)] = xs_flip

        def spread_bias(i):
            teb2_ps = ps_one.tile([P, D], F32, tag="spread")
            nc.tensor.matmul(
                teb2_ps[:], lhsT=sel[:, i].rearrange("q e b p -> q (e b p)"), rhs=vec_rows[:], start=True, stop=True
            )
            pair_tiles[("teb2", i)] = teb2_ps

        def add_task_embedding(i):
            xs_grouped = prep.tile([P, 2 * BATCH, TASKS, PACK], BF16, align_bytes=64)
            nc.vector.tensor_tensor(
                out=xs_grouped[:],
                in0=pair_tiles[("xs_flip", i)][:].rearrange("q t (s p) -> q s p t", p=TASKS),
                in1=te_col[:].unsqueeze(1).to_broadcast([P, 2 * BATCH, TASKS, PACK]),
                op=ALU.add,
            )
            pair_tiles[("xs_grouped", i)] = xs_grouped

        def residual_term(i):
            resid = prep.tile([P, D], F32)
            nc.vector.tensor_tensor(out=resid[:], in0=pair_tiles[("teb2", i)][:], in1=x_all[:, i, :], op=ALU.add)
            pair_tiles[("resid", i)] = resid

        def quantise_xs(i):
            xs_codes = prep.tile([P, 2 * SLOTS], U32, align_bytes=64)
            xs_scales = prep.tile([P, 2 * SLOTS], U8, align_bytes=64)
            quantise(nc, xs_codes[:], xs_scales[:], pair_tiles[("xs_grouped", i)][:].rearrange("q s p t -> q (s p t)"))
            xs_packed[i] = (xs_codes, xs_scales)

        def spread_gain(i, e):
            if e == 0:
                pair_tiles[("gb_wide", i)] = prep.tile([P, 2 * (D // P), 2, BATCH, TASKS], BF16, name="gb_wide")
            nc.scalar.copy(
                out=pair_tiles[("gb_wide", i)][:, :, e],
                in_=gb_col[:]
                .rearrange("q v c n p -> q (v c) n p")[:, :, 2 * i + e, :]
                .unsqueeze(2)
                .to_broadcast([P, 2 * (D // P), BATCH, TASKS]),
            )

        def flip_gain(i):
            gb_wide = pair_tiles[("gb_wide", i)]
            gb_ps = ps_two.tile([P, 2, D], BF16, tag="gb")
            for v in range(2):
                for c in range(D // P):
                    nc.tensor.transpose(
                        gb_ps[:, v, c * P : (c + 1) * P],
                        gb_wide[:, v * (D // P) + c].rearrange("q e b p -> q (e b p)"),
                        ident[:],
                    )
            pair_tiles[("gb", i)] = gb_ps

        def first_matmul(n):
            h_tiles[("h_ps", n)] = ps_two.tile([P, H_TILES, SLOTS], F32, tag="h", name="h_ps")
            codes, scales = w_packed[(1, n)]
            xs_codes, xs_scales = xs_packed[n // 2]
            mine = slice((n % 2) * SLOTS, (n % 2 + 1) * SLOTS)
            for m in range(H_TILES):
                nc.tensor.matmul_mx(
                    out=h_tiles[("h_ps", n)][:, m, :],
                    lhsT=codes[:, m * P : (m + 1) * P].bitcast(FP8X4),
                    lhsT_scale=scales[:, m * P : (m + 1) * P],
                    rhs=xs_codes[:, mine].bitcast(FP8X4),
                    rhs_scale=xs_scales[:, mine],
                    start=True,
                    stop=True,
                )

        def add_bias(n):
            pre = hid.tile([P, K2_PASSES, SLOTS, PACK], F32)
            nc.vector.tensor_tensor(
                out=pre[:],
                in0=h_tiles[("h_ps", n)][:].rearrange("q (g t) r -> q g r t", t=PACK),
                in1=b1_col[:, n].unsqueeze(2).to_broadcast([P, K2_PASSES, SLOTS, PACK]),
                op=ALU.add,
            )
            h_tiles[("pre", n)] = pre

        def silu(n):
            h_grouped = hid.tile([P, K2_PASSES, SLOTS, PACK], BF16, align_bytes=64)
            nc.scalar.activation(out=h_grouped[:], in_=h_tiles[("pre", n)][:], func=ACT.Silu)
            h_tiles[("grouped", n)] = h_grouped

        def second_matmul(n):
            i, e = divmod(n, 2)
            h_codes, h_scales = h_packed[e][i % 2]
            mine = slice(e * SLOTS, (e + 1) * SLOTS)
            for g in range(K2_PASSES):
                quantise(
                    nc,
                    h_codes[:, g, mine],
                    h_scales[:, g, mine],
                    h_tiles[("grouped", n)][:, g].rearrange("q r t -> q (r t)"),
                )
            if e == 0:
                pair_tiles[("mlp", i)] = ps_two.tile([P, D], F32, tag="mlp", name="mlp_ps")
            for g in range(K2_PASSES):
                codes, scales = w_packed[(2, n)]
                cols = slice(g * D, (g + 1) * D)
                nc.tensor.matmul_mx(
                    out=pair_tiles[("mlp", i)][:],
                    lhsT=h_codes[:, g].bitcast(FP8X4),
                    lhsT_scale=h_scales[:, g],
                    rhs=codes[:, cols].bitcast(FP8X4),
                    rhs_scale=scales[:, cols],
                    start=(e == 0 and g == 0),
                    stop=(e == 1 and g == K2_PASSES - 1),
                )

        def add_residual(i):
            r = norm.tile([P, D], F32)
            r_sum = norm.tile([P, 1], F32)
            nc.vector.scalar_tensor_tensor(
                out=r[:],
                in0=pair_tiles[("mlp", i)][:],
                scalar=1.0,
                in1=pair_tiles[("resid", i)][:],
                op0=ALU.mult,
                op1=ALU.add,
                accum_out=r_sum[:],
            )
            pair_tiles[("r", i)] = r
            pair_tiles[("r_sum", i)] = r_sum

        def negate_mean(i):
            neg_mean = norm.tile([P, 1], F32)
            nc.scalar.mul(neg_mean[:], pair_tiles[("r_sum", i)][:], -1.0 / D)
            pair_tiles[("neg_mean", i)] = neg_mean

        def variance(i):
            squares = norm.tile([P, D], F32)
            sq_sum = norm.tile([P, 1], F32)
            nc.scalar.activation(
                out=squares[:],
                in_=pair_tiles[("r", i)][:],
                func=ACT.Square,
                bias=pair_tiles[("neg_mean", i)][:],
                scale=1.0,
                accum_out=sq_sum[:],
            )
            pair_tiles[("sq_sum", i)] = sq_sum

        def inverse_deviation(i):
            var_eps = norm.tile([P, 1], F32)
            nc.scalar.activation(
                out=var_eps[:], in_=pair_tiles[("sq_sum", i)][:], func=ACT.Identity, scale=1.0 / D, bias=EPS
            )
            pair_tiles[("var_eps", i)] = var_eps

        def inverse_root_on_scalar(i):
            rstd = norm.tile([P, 1], F32)
            nc.scalar.activation(
                out=rstd[:], in_=pair_tiles[("sq_sum", i)][:], func=ACT.Abs_reciprocal_sqrt, scale=1.0 / D, bias=EPS
            )
            pair_tiles[("rstd", i)] = rstd

        def inverse_root(i):
            rstd = norm.tile([P, 1], F32)
            nc.gpsimd.tensor_tensor(out=rstd[:], in0=pair_tiles[("var_eps", i)][:], in1=neg_half[:], op=ALU.pow)
            pair_tiles[("rstd", i)] = rstd

        def centre_times_gain(i):
            scaled = norm.tile([P, D], F32)
            nc.vector.scalar_tensor_tensor(
                out=scaled[:],
                in0=pair_tiles[("r", i)][:],
                scalar=pair_tiles[("neg_mean", i)][:],
                in1=pair_tiles[("gb", i)][:, 0, :],
                op0=ALU.add,
                op1=ALU.mult,
            )
            pair_tiles[("scaled", i)] = scaled

        def normalise_and_store(i):
            y = norm.tile([P, D], F32)
            nc.vector.scalar_tensor_tensor(
                out=y[:],
                in0=pair_tiles[("scaled", i)][:],
                scalar=pair_tiles[("rstd", i)][:],
                in1=pair_tiles[("gb", i)][:, 1, :],
                op0=ALU.mult,
                op1=ALU.add,
            )
            for e in range(2):
                nc.sync.dma_start(out=out[:, 2 * i + e], in_=y[e * SLOTS : (e + 1) * SLOTS, :])

        regroup_piece(1, 0, 0)
        turn_task_embedding()
        flip_xs(0)
        spread_bias(0)
        regroup_piece(1, 0, 1)
        add_task_embedding(0)
        for n in range(EXPERTS):
            even = n % 2 == 0
            if n + PREFETCH < EXPERTS:
                load_w2(n + PREFETCH)
            if n + PREFETCH + 2 < EXPERTS:
                load_w1(n + PREFETCH + 2)

            if n + 1 < EXPERTS:
                regroup_piece(1, n + 1, 0)
            if even:
                quantise_xs(n // 2)
            quantise_weight(1, n)
            first_matmul(n)
            if n + 2 < EXPERTS:
                gpsimd_share(1, n + 2)
            if even and 4 <= n < EXPERTS - 2:
                inverse_root(n // 2 - 2)
            if even and n + 2 < EXPERTS:
                flip_xs(n // 2 + 1)
            if not even and n + 1 < EXPERTS:
                spread_bias(n // 2 + 1)
            if not even and n >= 3:
                flip_gain(n // 2 - 1)
            if n >= 1:
                silu(n - 1)
            for piece in range(len(w_raw[(2, n)])):
                regroup_piece(2, n, piece)
            if n == EXPERTS - 2:
                inverse_root(n // 2 - 2)
            if n == 0:
                turn_vectors()

            if not even and n >= 5:
                normalise_and_store(n // 2 - 2)
            if not even and n >= 3:
                add_residual(n // 2 - 1)
            if even and n >= 4:
                centre_times_gain(n // 2 - 2)
            if n == 0:
                residual_term(0)
            if not even and n + 1 < EXPERTS:
                residual_term(n // 2 + 1)
            add_bias(n)
            if even and n + 2 < EXPERTS:
                add_task_embedding(n // 2 + 1)

            if n >= 1:
                quantise_weight(2, n - 1)
                second_matmul(n - 1)
            if not even and n >= 3:
                negate_mean(n // 2 - 1)
            if not even:
                spread_gain(n // 2, 0)
            if n == EXPERTS - 1:
                silu(n)
            if not even and n >= 3:
                variance(n // 2 - 1)
            if not even:
                spread_gain(n // 2, 1)
            if not even and n >= 3 and n < EXPERTS - 1:
                inverse_deviation(n // 2 - 1)

        last = EXPERTS - 1
        inverse_root_on_scalar(PAIRS - 2)
        quantise_weight(2, last)
        second_matmul(last)
        flip_gain(PAIRS - 1)
        centre_times_gain(PAIRS - 2)
        add_residual(PAIRS - 1)
        negate_mean(PAIRS - 1)
        variance(PAIRS - 1)
        inverse_root_on_scalar(PAIRS - 1)
        normalise_and_store(PAIRS - 2)
        centre_times_gain(PAIRS - 1)
        normalise_and_store(PAIRS - 1)
